import numpy as np
import ml_dtypes


def mxq(x, axis, fmt="e4m3"):
    dtype, down = {"e4m3": (ml_dtypes.float8_e4m3fn, 7), "e5m2": (ml_dtypes.float8_e5m2, 14)}[fmt]
    v = np.moveaxis(np.asarray(x, np.float32).astype(ml_dtypes.bfloat16).astype(np.float64), axis, -1)
    blocks = v.reshape(v.shape[:-1] + (-1, 32))
    amax = np.abs(blocks).max(-1, keepdims=True)
    byte = np.maximum(np.where(amax > 0, np.frexp(amax)[1] - 1 + 127, 0) - down, 1)
    scale = np.exp2(byte - 127.0)
    codes = (blocks / scale).astype(np.float32).astype(dtype).astype(np.float64)
    return np.moveaxis((codes * scale).reshape(v.shape), -1, axis)


WIDE = False


def mx_kscale(k):
    if not WIDE:
        return np.ones(k)
    levels = np.array([30, -30])
    if k % 512:
        return np.exp2(np.random.permutation(np.resize(levels, k // 32))).repeat(32)
    a = np.empty((k // 512, 16))
    for p in range(k // 512):
        a[p, :8] = np.random.permutation(np.resize(levels, 8))
        for g in range(8):
            far = levels[np.abs(levels - a[p, g]) >= 10]
            a[p, g + 8] = far[np.random.randint(len(far))]
    return np.exp2(a.ravel()).repeat(32)


BF16 = ml_dtypes.bfloat16


def bf(x):
    return np.asarray(x, np.float32).astype(BF16)


def f64(x):
    return np.asarray(x).astype(np.float64)


B, I, H, P = 512, 1024, 1024, 2048


def sigmoid(v):
    return 1.0 / (1.0 + np.exp(-v))


def setup_inputs():
    s = mx_kscale(H)
    s = s * np.exp2(-np.round(np.log2(s.mean())))
    return {"hidden_new": bf((1.6 + 1.5 * np.random.standard_normal((B, H))) * s),
            "persistent_memory": bf(0.2 * np.random.standard_normal((B, P))),
            "Waddr": bf(np.random.standard_normal((P, H)) * 3.0 / np.sqrt(H) / s[None, :]),
            "baddr": bf(np.random.standard_normal(P)),
            "Wwrite": bf(np.random.standard_normal((P, H)) * 0.7 / np.sqrt(H) / s[None, :]),
            "bwrite": bf(np.random.standard_normal(P)),
            "Wforget": bf(np.random.standard_normal((P, H)) * 0.7 / np.sqrt(H) / s[None, :]),
            "bforget": bf(1.0 + 0.3 * np.random.standard_normal(P))}


def reference(hidden_new, persistent_memory, Waddr, baddr, Wwrite, bwrite, Wforget, bforget):
    hn = f64(hidden_new)
    hq = mxq(hn, 1, "e5m2")
    z = (hq @ mxq(f64(Waddr), 1, "e4m3").T) + f64(baddr)
    e = np.exp(z - z.max(axis=1, keepdims=True))
    addr = e / e.sum(axis=1, keepdims=True)
    write = sigmoid((hq @ mxq(f64(Wwrite), 1, "e4m3").T) + f64(bwrite))
    forget = sigmoid((hq @ mxq(f64(Wforget), 1, "e4m3").T) + f64(bforget))
    hp = np.mean(hn, axis=1, keepdims=True)
    return forget * f64(persistent_memory) + write * hp * addr

@@ -1,0 +1,450 @@
+from contextlib import ExitStack
+
+import concourse.mybir as mybir
+from concourse.masks import make_identity
+
+B, H, NSLOT = 512, 1024, 2048
+FLOPS = 3 * 2 * B * H * NSLOT
+
+F32 = mybir.dt.float32
+BF16 = mybir.dt.bfloat16
+U32 = mybir.dt.uint32
+U8 = mybir.dt.uint8
+E4M3 = mybir.dt.float8_e4m3fn_x4
+E5M2 = mybir.dt.float8_e5m2_x4
+ALU = mybir.AluOpType
+ACT = mybir.ActivationFunctionType
+AXIS_X = mybir.AxisListType.X
+
+P = 128
+PASSES = H // 512
+UNIT = 256
+TILES = UNIT // P
+NUNIT = NSLOT // UNIT
+NTOK = B // P
+BANKS = 8
+LAG = {'mx': 2, 'sigc': 2, 'rt': 4, 'appc': 4, 'bias': 3, 'act': 4, 'appr': 5, 'fin': 5}
+RUN = 1
+LAG2 = {'mx': 1, 'sigc': 1, 'rt': 2, 'appc': 2, 'bias': 1, 'act': 1, 'appr': 2, 'fin': 2}
+SWITCH = 18
+W_STATIONARY = [('forget', 1), ('forget', 3), ('forget', 5), ('forget', 7), ('write', 0), ('write', 1), ('write', 2), ('write', 3), ('write', 4), ('write', 5), ('write', 6), ('write', 7)]
+ORDER = [('hidden', 0), ('addr', 0), ('hidden', 1), ('addr', 1), ('addr', 2), ('forget', 0), ('addr', 3), ('forget', 1), ('addr', 4), ('forget', 2), ('addr', 5), ('forget', 3), ('addr', 6), ('forget', 4), ('addr', 7), ('forget', 5), ('forget', 6), ('forget', 7), ('write', 0), ('write', 1), ('write', 2), ('write', 3), ('write', 4), ('write', 5), ('write', 6), ('write', 7)]
+
+
+def tile_persistentgrucell_pc_kernel(
+    tc, hidden_new, persistent_memory, Waddr, baddr, Wwrite, bwrite, Wforget, bforget, out
+):
+    nc = tc.nc
+    weights = {"addr": Waddr, "write": Wwrite, "forget": Wforget}
+    biases = {"addr": baddr, "write": bwrite, "forget": bforget}
+
+    units = ORDER
+
+    def w_stationary(kind, u):
+        return (kind, u) in W_STATIONARY
+
+    with ExitStack() as ctx:
+        keep = ctx.enter_context(tc.tile_pool(name="keep", bufs=1))
+        rawp = ctx.enter_context(tc.tile_pool(name="rawp", bufs=10))
+        work = ctx.enter_context(tc.tile_pool(name="work", bufs=4))
+        psum = ctx.enter_context(tc.psum_pool(name="psum", bufs=1))
+        ctx.enter_context(tc.manual_schedule())
+
+        ident = keep.tile([P, P], F32)
+        make_identity(nc, ident[:])
+
+        h_raw = keep.tile([P, NTOK, H], BF16)
+        h_codes = keep.tile([P, PASSES, B], U32, align_bytes=64)
+        h_scales = keep.tile([P, PASSES, B], U8, align_bytes=64)
+        memory = keep.tile([P, NTOK, NSLOT], BF16)
+        expo = keep.tile([P, NUNIT, NTOK, UNIT], F32)
+        h_sum = keep.tile([P, NTOK], F32)
+        neg_max = keep.tile([P, NTOK, NUNIT], F32)
+        exp_sum = keep.tile([P, NTOK, NUNIT], F32)
+        unit_gap = keep.tile([P, NTOK, NUNIT], F32)
+        unit_factor = keep.tile([P, NTOK, NUNIT], F32)
+        unit_weight = keep.tile([P, NTOK, NUNIT], F32)
+        row_neg_max = keep.tile([P, NTOK], F32)
+        row_total = keep.tile([P, NTOK], F32)
+        row_inverse = keep.tile([P, NTOK], F32)
+        row_factor = keep.tile([P, NTOK], F32)
+        coef = keep.tile([P, NTOK, NUNIT], F32)
+        bias_rows = {}
+        for kind in ("addr", "forget", "write"):
+            if not all(w_stationary(kind, u) for u in range(NUNIT)):
+                bias_rows[kind] = keep.tile([P, NSLOT], BF16, name="bias_row_" + kind)
+        ident_bf = keep.tile([P, P], BF16)
+        make_identity(nc, ident_bf[:])
+        bias_lines = keep.tile([P, P], BF16)
+        nc.gpsimd.memset(bias_lines[:], 0.0)
+        bias_cols = keep.tile([P, 2, NSLOT // P], F32)
+        forget_term = keep.tile([P, NUNIT, NTOK, UNIT], F32)
+
+        state = {}
+        pending = []
+
+        def small_step():
+            if pending:
+                pending.pop(0)()
+
+        bank_count = [0]
+
+        def next_bank():
+            tag = "bank%d" % (bank_count[0] % BANKS)
+            bank_count[0] += 1
+            return psum.tile([P, 512], F32, name=tag, tag=tag)
+
+        def load(i):
+            kind, u = units[i]
+            if kind == "hidden":
+                for j in range(TILES):
+                    t = TILES * u + j
+                    nc.sync.dma_start(out=h_raw[:, t, :], in_=hidden_new[t * P : (t + 1) * P, :])
+                state[i, "raw"] = h_raw[:, TILES * u : TILES * (u + 1), :]
+                return
+            raw = rawp.tile([P, TILES, H], BF16, name="raw")
+            rows = weights[kind][u * UNIT : (u + 1) * UNIT, :]
+            nc.sync.dma_start(out=raw[:], in_=rows.rearrange("(j p) k -> p j k", j=TILES))
+            state[i, "raw"] = raw
+
+        def load_bias_row(kind, lo, hi):
+            nc.sync.dma_start(out=bias_rows[kind][:, lo:hi], in_=biases[kind][lo:hi].partition_broadcast(P))
+
+        lines = NSLOT // P
+
+        def load_bias_lines():
+            nc.sync.dma_start(out=bias_lines[0:lines, :], in_=bforget.rearrange("(c p) -> c p", p=P))
+            nc.sync.dma_start(out=bias_lines[lines : 2 * lines, :], in_=bwrite.rearrange("(c p) -> c p", p=P))
+
+        def turn_bias_lines():
+            tag = "bank%d" % (bank_count[0] % BANKS)
+            bank_count[0] += 1
+            turned = psum.tile([P, P], BF16, name=tag, tag=tag)
+            nc.tensor.transpose(turned[:], bias_lines[:], ident_bf[:])
+            nc.vector.tensor_scalar(
+                out=bias_cols[:, 0, :], in0=turned[:, 0:lines], scalar1=0.5, scalar2=None, op0=ALU.mult
+            )
+            nc.vector.tensor_copy(out=bias_cols[:, 1, :], in_=turned[:, lines : 2 * lines])
+
+        def load_memory(lo, hi):
+            nc.sync.dma_start(
+                out=memory[:, :, lo:hi],
+                in_=persistent_memory[:, lo:hi].rearrange("(t p) c -> p t c", p=P),
+            )
+
+        def transpose_rows(i):
+            raw = state[i, "raw"]
+            banks = []
+            for j in range(TILES):
+                words = raw[:, j, :].bitcast(F32)
+                bank = next_bank()
+                view = bank[:].rearrange("p (g v r) -> p g v r", g=PASSES, v=2)
+                for g in range(PASSES):
+                    for v in range(2):
+                        nc.tensor.transpose(view[:, g, v, :], words[:, 256 * g + v : 256 * (g + 1) : 2], ident[:])
+                banks.append(bank)
+            state[i, "tbanks"] = banks
+
+        def copy_rows(i):
+            grouped = work.tile([P, PASSES * UNIT * 4], BF16, name="grouped", align_bytes=64)
+            words = grouped[:].bitcast(F32).rearrange("p (g r v) -> p g r v", g=PASSES, v=2)
+            for j in range(TILES):
+                src = state[i, "tbanks"][j][:].rearrange("p (g v r) -> p g r v", g=PASSES, v=2)
+                nc.scalar.copy(out=words[:, :, j * P : (j + 1) * P, :], in_=src)
+            state[i, "grouped"] = grouped
+
+        def quantize(i):
+            kind, u = units[i]
+            grouped = state[i, "grouped"]
+            if kind == "hidden":
+                cols = slice(u * UNIT, (u + 1) * UNIT)
+                for g in range(PASSES):
+                    nc.vector.quantize_mx(
+                        out=h_codes[:, g, cols].bitcast(E5M2),
+                        scales=h_scales[:, g, cols],
+                        in_=grouped[:, g * UNIT * 4 : (g + 1) * UNIT * 4],
+                    )
+                state["hq", u] = True
+                return
+            w_codes = work.tile([P, PASSES * UNIT], U32, name="w_codes", align_bytes=64)
+            w_scales = work.tile([P, PASSES * UNIT], U8, name="w_scales", align_bytes=64)
+            nc.vector.quantize_mx(out=w_codes[:].bitcast(E4M3), scales=w_scales[:], in_=grouped[:])
+            state[i, "codes"] = (w_codes, w_scales)
+            small_step()
+
+        def multiply(i):
+            kind, u = units[i]
+            w_codes, w_scales = state[i, "codes"]
+            banks = []
+            for b in range(2):
+                bank = next_bank()
+                if w_stationary(kind, u):
+                    for g in range(PASSES):
+                        cols = slice(g * UNIT + b * P, g * UNIT + (b + 1) * P)
+                        nc.tensor.matmul_mx(
+                            out=bank[:],
+                            lhsT=w_codes[:, cols].bitcast(E4M3),
+                            lhsT_scale=w_scales[:, cols],
+                            rhs=h_codes[:, g, :].bitcast(E5M2),
+                            rhs_scale=h_scales[:, g, :],
+                            start=(g == 0),
+                            stop=(g == PASSES - 1),
+                        )
+                else:
+                    for tt in range(2):
+                        t = 2 * b + tt
+                        for g in range(PASSES):
+                            cols = slice(g * UNIT, (g + 1) * UNIT)
+                            nc.tensor.matmul_mx(
+                                out=bank[:, tt * UNIT : (tt + 1) * UNIT],
+                                lhsT=h_codes[:, g, t * P : (t + 1) * P].bitcast(E5M2),
+                                lhsT_scale=h_scales[:, g, t * P : (t + 1) * P],
+                                rhs=w_codes[:, cols].bitcast(E4M3),
+                                rhs_scale=w_scales[:, cols],
+                                start=(g == 0),
+                                stop=(g == PASSES - 1),
+                            )
+                banks.append(bank)
+            state[i, "mbanks"] = banks
+
+        def add_bias(i):
+            kind, u = units[i]
+            bias = bias_rows[kind][:, u * UNIT : (u + 1) * UNIT].unsqueeze(1).broadcast_to([P, 2, UNIT])
+            if kind != "addr":
+                gate = work.tile([P, NTOK, UNIT], F32, name="gate")
+                state[i, "gate"] = gate
+            for b in range(2):
+                sums = state[i, "mbanks"][b][:].rearrange("p (t c) -> p t c", t=2)
+                if kind == "addr":
+                    nc.vector.scalar_tensor_tensor(
+                        out=expo[:, u, 2 * b : 2 * b + 2, :], in0=sums, scalar=-1.0, in1=bias,
+                        op0=ALU.mult, op1=ALU.subtract,
+                    )
+                else:
+                    nc.vector.tensor_tensor(out=gate[:, 2 * b : 2 * b + 2, :], in0=sums, in1=bias, op=ALU.add)
+                small_step()
+
+        def unit_max(i):
+            kind, u = units[i]
+            for b in range(2):
+                nc.vector.tensor_reduce(
+                    out=neg_max[:, 2 * b : 2 * b + 2, u], in_=expo[:, u, 2 * b : 2 * b + 2, :],
+                    axis=AXIS_X, op=ALU.min,
+                )
+
+        def exponentials(i):
+            kind, u = units[i]
+            for t in range(NTOK):
+                nc.scalar.activation(
+                    out=expo[:, u, t, :], in_=expo[:, u, t, :], func=ACT.Exp, scale=-1.0,
+                    bias=neg_max[:, t, u : u + 1], accum_out=exp_sum[:, t, u : u + 1],
+                )
+
+        def sigmoid_rows(i):
+            gate = state[i, "gate"]
+            for b in range(2):
+                rows = gate[:, 2 * b : 2 * b + 2, :]
+                if units[i][0] == "forget":
+                    nc.scalar.activation(out=rows, in_=rows, func=ACT.Tanh, scale=0.5)
+                else:
+                    nc.scalar.activation(out=rows, in_=rows, func=ACT.Sigmoid)
+
+        def sigmoid_cols(i):
+            kind, u = units[i]
+            gate_t = work.tile([P, TILES, B], F32, name="gate_t")
+            for j in range(TILES):
+                c = TILES * u + j
+                if kind == "forget":
+                    nc.scalar.activation(
+                        out=gate_t[:, j, :], in_=state[i, "mbanks"][j][:], func=ACT.Tanh, scale=0.5,
+                        bias=bias_cols[:, 0, c : c + 1],
+                    )
+                else:
+                    nc.scalar.activation(
+                        out=gate_t[:, j, :], in_=state[i, "mbanks"][j][:], func=ACT.Sigmoid,
+                        bias=bias_cols[:, 1, c : c + 1],
+                    )
+            state[i, "gate_t"] = gate_t
+
+        def transpose_gate(i):
+            gate_t = state[i, "gate_t"]
+            banks = []
+            for b in range(2):
+                bank = next_bank()
+                view = bank[:].rearrange("p (t j m) -> p t j m", t=2, j=TILES)
+                for tt in range(2):
+                    t = 2 * b + tt
+                    for j in range(TILES):
+                        nc.tensor.transpose(view[:, tt, j, :], gate_t[:, j, t * P : (t + 1) * P], ident[:])
+                banks.append(bank)
+            state[i, "gbanks"] = banks
+
+        def gate_view(i, b):
+            kind, u = units[i]
+            if w_stationary(kind, u):
+                return state[i, "gbanks"][b][:].rearrange("p (t c) -> p t c", t=2)
+            return state[i, "gate"][:, 2 * b : 2 * b + 2, :]
+
+        def apply_gate(i):
+            kind, u = units[i]
+            if kind == "write":
+                while pending:
+                    small_step()
+                write_term = work.tile([P, NTOK, UNIT], F32, name="write_term", bufs=3)
+                state["write", u] = write_term
+            for b in range(2):
+                gate = gate_view(i, b)
+                if kind == "forget":
+                    nc.vector.scalar_tensor_tensor(
+                        out=forget_term[:, u, 2 * b : 2 * b + 2, :],
+                        in0=gate,
+                        scalar=1.0,
+                        in1=memory[:, 2 * b : 2 * b + 2, u * UNIT : (u + 1) * UNIT],
+                        op0=ALU.add, op1=ALU.mult,
+                    )
+                    small_step()
+                else:
+                    for tt in range(2):
+                        t = 2 * b + tt
+                        nc.vector.scalar_tensor_tensor(
+                            out=write_term[:, t, :], in0=gate[:, tt, :], scalar=coef[:, t, u : u + 1],
+                            in1=expo[:, u, t, :], op0=ALU.mult, op1=ALU.mult,
+                        )
+
+        def finish(u):
+            for b in range(2):
+                rows = slice(2 * b, 2 * b + 2)
+                nc.vector.scalar_tensor_tensor(
+                    out=forget_term[:, u, rows, :], in0=forget_term[:, u, rows, :], scalar=0.5,
+                    in1=state["write", u][:, rows, :], op0=ALU.mult, op1=ALU.add,
+                )
+                nc.sync.dma_start(
+                    out=out[2 * b * P : (2 * b + 2) * P, u * UNIT : (u + 1) * UNIT].rearrange("(t p) c -> p t c", p=P),
+                    in_=forget_term[:, u, rows, :],
+                )
+
+        def spread(col):
+            return col.unsqueeze(2).broadcast_to([P, NTOK, NUNIT])
+
+        def softmax_gap():
+            pending.append(lambda: nc.vector.tensor_reduce(out=row_neg_max[:], in_=neg_max[:], axis=AXIS_X, op=ALU.min))
+            pending.append(lambda: nc.vector.tensor_tensor(
+                out=unit_gap[:], in0=spread(row_neg_max[:]), in1=neg_max[:], op=ALU.subtract))
+
+        def softmax_factor():
+            while pending:
+                small_step()
+            nc.scalar.activation(out=unit_factor[:], in_=unit_gap[:], func=ACT.Exp)
+
+        def softmax_coef():
+            pending.append(lambda: nc.vector.tensor_tensor(
+                out=unit_weight[:], in0=exp_sum[:], in1=unit_factor[:], op=ALU.mult))
+            pending.append(lambda: nc.vector.tensor_reduce(
+                out=row_total[:], in_=unit_weight[:], axis=AXIS_X, op=ALU.add))
+            pending.append(lambda: nc.vector.reciprocal(out=row_inverse[:], in_=row_total[:]))
+            pending.append(lambda: nc.vector.scalar_tensor_tensor(
+                out=row_factor[:], in0=row_inverse[:], scalar=1.0 / H, in1=h_sum[:], op0=ALU.mult, op1=ALU.mult))
+            pending.append(lambda: nc.vector.tensor_tensor(
+                out=coef[:], in0=unit_factor[:], in1=spread(row_factor[:]), op=ALU.mult))
+
+        def row_sums(u):
+            rows = slice(TILES * u, TILES * (u + 1))
+            nc.vector.tensor_reduce(out=h_sum[:, rows], in_=h_raw[:, rows, :], axis=AXIS_X, op=ALU.add)
+
+        n = len(units)
+        first_forget = units.index(("forget", 0))
+        last_addr = units.index(("addr", NUNIT - 1))
+
+        def kind_of(i):
+            return units[i][0] if 0 <= i < n else "none"
+
+        def is_weight(i):
+            return kind_of(i) in weights
+
+        def is_cols(i):
+            return is_weight(i) and w_stationary(units[i][0], units[i][1])
+
+        def is_rows(i):
+            return is_weight(i) and not is_cols(i)
+
+        def is_gate_rows(i):
+            return is_rows(i) and kind_of(i) != "addr"
+
+        ahead = 10
+        loaded = [0]
+
+        def load_up_to(limit):
+            while loaded[0] < min(limit, n):
+                i = loaded[0]
+                load(i)
+                kind, u = units[i]
+                if kind in bias_rows and u % 2 == 0 and not (w_stationary(kind, u) and w_stationary(kind, u + 1)):
+                    load_bias_row(kind, u * UNIT, (u + 2) * UNIT)
+                if i == 3:
+                    load_bias_lines()
+                if kind == "forget" and u % 4 == 0:
+                    load_memory(u * UNIT, (u + 4) * UNIT)
+                loaded[0] += 1
+
+        def due(stage, s):
+            return [i for i in range(n) if i + (LAG2 if i >= SWITCH else LAG)[stage] == s]
+
+        load_up_to(2 + ahead)
+        for s in range(n + max(LAG.values()) + 1):
+            if s % RUN == 0:
+                for r in range(RUN):
+                    if s + r < n:
+                        transpose_rows(s + r)
+                if s == 4:
+                    turn_bias_lines()
+                if s >= n:
+                    for r in range(RUN):
+                        for i in due("mx", s + r):
+                            if is_weight(i):
+                                multiply(i)
+                for r in range(RUN):
+                    for i in due("rt", s + r):
+                        if is_cols(i):
+                            transpose_gate(i)
+                if s < n:
+                    for r in range(RUN):
+                        for i in due("mx", s + r):
+                            if is_weight(i):
+                                multiply(i)
+            load_up_to(s + 1 + ahead)
+            if kind_of(s) == "hidden":
+                row_sums(units[s][1])
+            for i in due("bias", s):
+                if is_rows(i):
+                    add_bias(i)
+            for i in due("bias", s):
+                if kind_of(i) == "addr":
+                    unit_max(i)
+                if i == last_addr:
+                    softmax_gap()
+            if s < n:
+                copy_rows(s)
+            for i in due("act", s):
+                if kind_of(i) == "addr":
+                    exponentials(i)
+            if s - LAG["bias"] - 1 == last_addr:
+                softmax_factor()
+            for i in due("act", s):
+                if is_gate_rows(i):
+                    sigmoid_rows(i)
+            for i in due("sigc", s):
+                if is_cols(i):
+                    sigmoid_cols(i)
+            for i in due("appc", s):
+                if is_cols(i):
+                    apply_gate(i)
+            if s < n:
+                quantize(s)
+            if s - max(LAG["act"], LAG["bias"] + 1) == last_addr:
+                softmax_coef()
+            for i in due("appr", s):
+                if is_gate_rows(i):
+                    apply_gate(i)
+            for i in due("fin", s):
+                if kind_of(i) == "write":
+                    finish(units[i][1])

@@ -23,12 +23,17 @@ TILES = UNIT // P
 NUNIT = NSLOT // UNIT
 NTOK = B // P
 BANKS = 8
+LINE = 512
+LINES = NSLOT // LINE
+FIRST_LINE = {"addr": 0, "forget": LINES, "write": 2 * LINES}
 LAG = {'mx': 2, 'sigc': 2, 'rt': 4, 'appc': 4, 'bias': 3, 'act': 4, 'appr': 5, 'fin': 5}
 RUN = 1
+TANH_UNITS = 4
+EARLY = 0
 LAG2 = {'mx': 1, 'sigc': 1, 'rt': 2, 'appc': 2, 'bias': 1, 'act': 1, 'appr': 2, 'fin': 2}
-SWITCH = 18
+SWITCH = 17
 W_STATIONARY = [('forget', 1), ('forget', 3), ('forget', 5), ('forget', 7), ('write', 0), ('write', 1), ('write', 2), ('write', 3), ('write', 4), ('write', 5), ('write', 6), ('write', 7)]
-ORDER = [('hidden', 0), ('addr', 0), ('hidden', 1), ('addr', 1), ('addr', 2), ('forget', 0), ('addr', 3), ('forget', 1), ('addr', 4), ('forget', 2), ('addr', 5), ('forget', 3), ('addr', 6), ('forget', 4), ('addr', 7), ('forget', 5), ('forget', 6), ('forget', 7), ('write', 0), ('write', 1), ('write', 2), ('write', 3), ('write', 4), ('write', 5), ('write', 6), ('write', 7)]
+ORDER = [('hidden', 0), ('addr', 0), ('hidden', 1), ('addr', 1), ('addr', 2), ('addr', 3), ('addr', 4), ('forget', 0), ('addr', 5), ('forget', 1), ('addr', 6), ('forget', 2), ('addr', 7), ('forget', 3), ('forget', 4), ('forget', 5), ('forget', 6), ('forget', 7), ('write', 0), ('write', 1), ('write', 2), ('write', 3), ('write', 4), ('write', 5), ('write', 6), ('write', 7)]
 
 
 def tile_persistentgrucell_pc_kernel(
@@ -42,6 +47,9 @@ def tile_persistentgrucell_pc_kernel(
 
     def w_stationary(kind, u):
         return (kind, u) in W_STATIONARY
+
+    def by_tanh(kind, u):
+        return kind == "forget" and u < TANH_UNITS
 
     with ExitStack() as ctx:
         keep = ctx.enter_context(tc.tile_pool(name="keep", bufs=1))
@@ -75,9 +83,10 @@ def tile_persistentgrucell_pc_kernel(
                 bias_rows[kind] = keep.tile([P, NSLOT], BF16, name="bias_row_" + kind)
         ident_bf = keep.tile([P, P], BF16)
         make_identity(nc, ident_bf[:])
-        bias_lines = keep.tile([P, P], BF16)
-        nc.gpsimd.memset(bias_lines[:], 0.0)
+        bias_lines = keep.tile([P, LINE], BF16)
+        nc.vector.memset(bias_lines[:], 0.0)
         bias_cols = keep.tile([P, 2, NSLOT // P], F32)
+        half_cols = keep.tile([P, NSLOT // P], F32)
         forget_term = keep.tile([P, NUNIT, NTOK, UNIT], F32)
 
         state = {}
@@ -107,24 +116,51 @@ def tile_persistentgrucell_pc_kernel(
             nc.sync.dma_start(out=raw[:], in_=rows.rearrange("(j p) k -> p j k", j=TILES))
             state[i, "raw"] = raw
 
-        def load_bias_row(kind, lo, hi):
-            nc.sync.dma_start(out=bias_rows[kind][:, lo:hi], in_=biases[kind][lo:hi].partition_broadcast(P))
-
-        lines = NSLOT // P
-
         def load_bias_lines():
-            nc.sync.dma_start(out=bias_lines[0:lines, :], in_=bforget.rearrange("(c p) -> c p", p=P))
-            nc.sync.dma_start(out=bias_lines[lines : 2 * lines, :], in_=bwrite.rearrange("(c p) -> c p", p=P))
+            for kind in ("addr", "forget", "write"):
+                first = FIRST_LINE[kind]
+                nc.scalar.dma_start(
+                    out=bias_lines[first : first + LINES, :], in_=biases[kind].rearrange("(c n) -> c n", n=LINE)
+                )
+
+        def spread_bias(kind, unit_list, copy):
+            bank = next_bank()
+            for k, u in enumerate(unit_list):
+                line = FIRST_LINE[kind] + u // 2
+                nc.tensor.matmul(
+                    bank[:, k * UNIT : (k + 1) * UNIT],
+                    lhsT=ident_bf[:, line : line + 1].to_broadcast([P, P]),
+                    rhs=bias_lines[:, (u % 2) * UNIT : (u % 2 + 1) * UNIT],
+                    start=True, stop=True,
+                )
+            for k, u in enumerate(unit_list):
+                copy(out=bias_rows[kind][:, u * UNIT : (u + 1) * UNIT], in_=bank[:, k * UNIT : (k + 1) * UNIT])
+
+        def spread_line(kind, c, copy):
+            bank = next_bank()
+            line = FIRST_LINE[kind] + c
+            nc.tensor.matmul(
+                bank[:], lhsT=ident_bf[:, line : line + 1].to_broadcast([P, P]), rhs=bias_lines[:],
+                start=True, stop=True,
+            )
+            copy(out=bias_rows[kind][:, c * LINE : (c + 1) * LINE], in_=bank[:])
 
         def turn_bias_lines():
             tag = "bank%d" % (bank_count[0] % BANKS)
             bank_count[0] += 1
-            turned = psum.tile([P, P], BF16, name=tag, tag=tag)
-            nc.tensor.transpose(turned[:], bias_lines[:], ident_bf[:])
-            nc.vector.tensor_scalar(
-                out=bias_cols[:, 0, :], in0=turned[:, 0:lines], scalar1=0.5, scalar2=None, op0=ALU.mult
-            )
-            nc.vector.tensor_copy(out=bias_cols[:, 1, :], in_=turned[:, lines : 2 * lines])
+            turned = psum.tile([P, LINE // P, P], BF16, name=tag, tag=tag)
+            for j in range(LINE // P):
+                nc.tensor.transpose(turned[:, j, :], bias_lines[:, j * P : (j + 1) * P], ident_bf[:])
+            views = {}
+            for kind in ("forget", "write"):
+                first = FIRST_LINE[kind]
+                views[kind] = turned[:, :, first : first + LINES].rearrange("p j c -> p c j")
+            cols = bias_cols[:].rearrange("p g (c j) -> p g c j", j=LINE // P)
+            halves = half_cols[:].rearrange("p (c j) -> p c j", j=LINE // P)
+            nc.vector.tensor_scalar(out=halves, in0=views["forget"], scalar1=0.5, scalar2=None, op0=ALU.mult)
+            if TANH_UNITS < NUNIT:
+                nc.vector.tensor_copy(out=cols[:, 0], in_=views["forget"])
+            nc.vector.tensor_copy(out=cols[:, 1], in_=views["write"])
 
         def load_memory(lo, hi):
             nc.sync.dma_start(
@@ -172,11 +208,11 @@ def tile_persistentgrucell_pc_kernel(
             state[i, "codes"] = (w_codes, w_scales)
             small_step()
 
-        def multiply(i):
+        def multiply(i, halves=(0, 1)):
             kind, u = units[i]
             w_codes, w_scales = state[i, "codes"]
-            banks = []
-            for b in range(2):
+            banks = state.setdefault((i, "mbanks"), [])
+            for b in halves:
                 bank = next_bank()
                 if w_stationary(kind, u):
                     for g in range(PASSES):
@@ -205,7 +241,6 @@ def tile_persistentgrucell_pc_kernel(
                                 stop=(g == PASSES - 1),
                             )
                 banks.append(bank)
-            state[i, "mbanks"] = banks
 
         def add_bias(i):
             kind, u = units[i]
@@ -244,7 +279,7 @@ def tile_persistentgrucell_pc_kernel(
             gate = state[i, "gate"]
             for b in range(2):
                 rows = gate[:, 2 * b : 2 * b + 2, :]
-                if units[i][0] == "forget":
+                if by_tanh(units[i][0], units[i][1]):
                     nc.scalar.activation(out=rows, in_=rows, func=ACT.Tanh, scale=0.5)
                 else:
                     nc.scalar.activation(out=rows, in_=rows, func=ACT.Sigmoid)
@@ -254,15 +289,15 @@ def tile_persistentgrucell_pc_kernel(
             gate_t = work.tile([P, TILES, B], F32, name="gate_t")
             for j in range(TILES):
                 c = TILES * u + j
-                if kind == "forget":
+                if by_tanh(kind, u):
                     nc.scalar.activation(
                         out=gate_t[:, j, :], in_=state[i, "mbanks"][j][:], func=ACT.Tanh, scale=0.5,
-                        bias=bias_cols[:, 0, c : c + 1],
+                        bias=half_cols[:, c : c + 1],
                     )
                 else:
                     nc.scalar.activation(
                         out=gate_t[:, j, :], in_=state[i, "mbanks"][j][:], func=ACT.Sigmoid,
-                        bias=bias_cols[:, 1, c : c + 1],
+                        bias=bias_cols[:, 0 if kind == "forget" else 1, c : c + 1],
                     )
             state[i, "gate_t"] = gate_t
 
@@ -298,7 +333,7 @@ def tile_persistentgrucell_pc_kernel(
                     nc.vector.scalar_tensor_tensor(
                         out=forget_term[:, u, 2 * b : 2 * b + 2, :],
                         in0=gate,
-                        scalar=1.0,
+                        scalar=1.0 if by_tanh(kind, u) else 0.0,
                         in1=memory[:, 2 * b : 2 * b + 2, u * UNIT : (u + 1) * UNIT],
                         op0=ALU.add, op1=ALU.mult,
                     )
@@ -315,7 +350,7 @@ def tile_persistentgrucell_pc_kernel(
             for b in range(2):
                 rows = slice(2 * b, 2 * b + 2)
                 nc.vector.scalar_tensor_tensor(
-                    out=forget_term[:, u, rows, :], in0=forget_term[:, u, rows, :], scalar=0.5,
+                    out=forget_term[:, u, rows, :], in0=forget_term[:, u, rows, :], scalar=0.5 if by_tanh("forget", u) else 1.0,
                     in1=state["write", u][:, rows, :], op0=ALU.mult, op1=ALU.add,
                 )
                 nc.sync.dma_start(
@@ -378,10 +413,6 @@ def tile_persistentgrucell_pc_kernel(
                 i = loaded[0]
                 load(i)
                 kind, u = units[i]
-                if kind in bias_rows and u % 2 == 0 and not (w_stationary(kind, u) and w_stationary(kind, u + 1)):
-                    load_bias_row(kind, u * UNIT, (u + 2) * UNIT)
-                if i == 3:
-                    load_bias_lines()
                 if kind == "forget" and u % 4 == 0:
                     load_memory(u * UNIT, (u + 4) * UNIT)
                 loaded[0] += 1
@@ -389,7 +420,12 @@ def tile_persistentgrucell_pc_kernel(
         def due(stage, s):
             return [i for i in range(n) if i + (LAG2 if i >= SWITCH else LAG)[stage] == s]
 
+        load_bias_lines()
         load_up_to(2 + ahead)
+        for c in range(LINES):
+            spread_line("addr", c, nc.scalar.copy if c % 2 == 0 else nc.vector.tensor_copy)
+        row_gates = [(kind, [u for u in range(NUNIT) if not w_stationary(kind, u)]) for kind in ("forget", "write")]
+        row_groups = [(kind, us[k : k + 2]) for kind, us in row_gates for k in range(0, len(us), 2)]
         for s in range(n + max(LAG.values()) + 1):
             if s % RUN == 0:
                 for r in range(RUN):
@@ -397,6 +433,8 @@ def tile_persistentgrucell_pc_kernel(
                         transpose_rows(s + r)
                 if s == 4:
                     turn_bias_lines()
+                if 1 <= s <= len(row_groups):
+                    spread_bias(row_groups[s - 1][0], row_groups[s - 1][1], nc.scalar.copy)
                 if s >= n:
                     for r in range(RUN):
                         for i in due("mx", s + r):
@@ -407,13 +445,15 @@ def tile_persistentgrucell_pc_kernel(
                         if is_cols(i):
                             transpose_gate(i)
                 if s < n:
+                    if EARLY and s == 2:
+                        multiply(1, (0,))
                     for r in range(RUN):
                         for i in due("mx", s + r):
                             if is_weight(i):
-                                multiply(i)
+                                multiply(i, (1,) if EARLY and i == 1 else (0, 1))
             load_up_to(s + 1 + ahead)
-            if kind_of(s) == "hidden":
-                row_sums(units[s][1])
+            if s == 0:
+                row_sums(0)
             for i in due("bias", s):
                 if is_rows(i):
                     add_bias(i)
@@ -440,6 +480,8 @@ def tile_persistentgrucell_pc_kernel(
                     apply_gate(i)
             if s < n:
                 quantize(s)
+            if units[min(s, n - 1)] == ("hidden", 1):
+                row_sums(1)
             if s - max(LAG["act"], LAG["bias"] + 1) == last_addr:
                 softmax_coef()
             for i in due("appr", s):

@@ -17,23 +17,28 @@ ACT = mybir.ActivationFunctionType
 AXIS_X = mybir.AxisListType.X
 
 P = 128
-PASSES = H // 512
+PACK = 4
+PASSES = H // (P * PACK)
+PASS_WORDS = P * PACK // 2
+BANK = 512
+BANKS = 8
 UNIT = 256
 TILES = UNIT // P
 NUNIT = NSLOT // UNIT
 NTOK = B // P
-BANKS = 8
-LINE = 512
-LINES = NSLOT // LINE
+PAIR = BANK // UNIT
+HALVES = NTOK // PAIR
+LINES = NSLOT // BANK
 FIRST_LINE = {"addr": 0, "forget": LINES, "write": 2 * LINES}
-LAG = {'mx': 2, 'sigc': 2, 'rt': 4, 'appc': 4, 'bias': 3, 'act': 4, 'appr': 5, 'fin': 5}
-RUN = 1
+
+ADDR_LEAD = 6
+FORGET_PERIOD = 4
 TANH_UNITS = 4
-EARLY = 0
-LAG2 = {'mx': 1, 'sigc': 1, 'rt': 2, 'appc': 2, 'bias': 1, 'act': 1, 'appr': 2, 'fin': 2}
-SWITCH = 17
-W_STATIONARY = [('forget', 1), ('forget', 3), ('forget', 5), ('forget', 7), ('write', 0), ('write', 1), ('write', 2), ('write', 3), ('write', 4), ('write', 5), ('write', 6), ('write', 7)]
-ORDER = [('hidden', 0), ('addr', 0), ('hidden', 1), ('addr', 1), ('addr', 2), ('addr', 3), ('addr', 4), ('forget', 0), ('addr', 5), ('forget', 1), ('addr', 6), ('forget', 2), ('addr', 7), ('forget', 3), ('forget', 4), ('forget', 5), ('forget', 6), ('forget', 7), ('write', 0), ('write', 1), ('write', 2), ('write', 3), ('write', 4), ('write', 5), ('write', 6), ('write', 7)]
+MULTIPLY_LAG = 2
+TURN_LAG = 2
+SHORT_FROM = 18
+RAW_BUFS = 10
+WORK_BUFS = 4
 
 
 def tile_persistentgrucell_pc_kernel(
@@ -43,450 +48,352 @@ def tile_persistentgrucell_pc_kernel(
     weights = {"addr": Waddr, "write": Wwrite, "forget": Wforget}
     biases = {"addr": baddr, "write": bwrite, "forget": bforget}
 
-    units = ORDER
+    units = [("hidden", 0), ("addr", 0), ("hidden", 1)]
+    units += [("addr", u) for u in range(1, ADDR_LEAD)]
+    for u in range(NUNIT):
+        units.append(("forget", u))
+        if ADDR_LEAD + u < NUNIT:
+            units.append(("addr", ADDR_LEAD + u))
+    units += [("write", u) for u in range(NUNIT)]
 
-    def w_stationary(kind, u):
-        return (kind, u) in W_STATIONARY
+    def slot_form(kind, u):
+        return kind == "write" or (kind == "forget" and u % FORGET_PERIOD == 1)
 
     def by_tanh(kind, u):
         return kind == "forget" and u < TANH_UNITS
 
+    def slots(u):
+        return slice(u * UNIT, (u + 1) * UNIT)
+
+    def pair(half):
+        return slice(PAIR * half, PAIR * (half + 1))
+
     with ExitStack() as ctx:
         keep = ctx.enter_context(tc.tile_pool(name="keep", bufs=1))
-        rawp = ctx.enter_context(tc.tile_pool(name="rawp", bufs=10))
-        work = ctx.enter_context(tc.tile_pool(name="work", bufs=4))
+        stream = ctx.enter_context(tc.tile_pool(name="stream", bufs=RAW_BUFS))
+        work = ctx.enter_context(tc.tile_pool(name="work", bufs=WORK_BUFS))
         psum = ctx.enter_context(tc.psum_pool(name="psum", bufs=1))
-        ctx.enter_context(tc.manual_schedule())
+        ctx.enter_context(tc.manual_schedule(engines={mybir.EngineType.PE, mybir.EngineType.SP}))
 
         ident = keep.tile([P, P], F32)
         make_identity(nc, ident[:])
+        ident_bf = keep.tile([P, P], BF16)
+        make_identity(nc, ident_bf[:])
 
         h_raw = keep.tile([P, NTOK, H], BF16)
         h_codes = keep.tile([P, PASSES, B], U32, align_bytes=64)
         h_scales = keep.tile([P, PASSES, B], U8, align_bytes=64)
+        h_sum = keep.tile([P, NTOK], F32)
         memory = keep.tile([P, NTOK, NSLOT], BF16)
         expo = keep.tile([P, NUNIT, NTOK, UNIT], F32)
-        h_sum = keep.tile([P, NTOK], F32)
         neg_max = keep.tile([P, NTOK, NUNIT], F32)
         exp_sum = keep.tile([P, NTOK, NUNIT], F32)
-        unit_gap = keep.tile([P, NTOK, NUNIT], F32)
-        unit_factor = keep.tile([P, NTOK, NUNIT], F32)
-        unit_weight = keep.tile([P, NTOK, NUNIT], F32)
-        row_neg_max = keep.tile([P, NTOK], F32)
-        row_total = keep.tile([P, NTOK], F32)
-        row_inverse = keep.tile([P, NTOK], F32)
-        row_factor = keep.tile([P, NTOK], F32)
         coef = keep.tile([P, NTOK, NUNIT], F32)
-        bias_rows = {}
-        for kind in ("addr", "forget", "write"):
-            if not all(w_stationary(kind, u) for u in range(NUNIT)):
-                bias_rows[kind] = keep.tile([P, NSLOT], BF16, name="bias_row_" + kind)
-        ident_bf = keep.tile([P, P], BF16)
-        make_identity(nc, ident_bf[:])
-        bias_lines = keep.tile([P, LINE], BF16)
+        result = keep.tile([P, NUNIT, NTOK, UNIT], F32)
+
+        bias_lines = keep.tile([P, BANK], BF16)
         nc.vector.memset(bias_lines[:], 0.0)
-        bias_cols = keep.tile([P, 2, NSLOT // P], F32)
-        half_cols = keep.tile([P, NSLOT // P], F32)
-        forget_term = keep.tile([P, NUNIT, NTOK, UNIT], F32)
+        addr_bias = keep.tile([P, NSLOT], BF16)
+        forget_bias = keep.tile([P, NSLOT], BF16)
+        row_bias = {"addr": addr_bias, "forget": forget_bias}
+        col_bias = keep.tile([P, BANK // P, 3 * LINES], F32)
+        half_bias = keep.tile([P, BANK // P, LINES], F32)
 
-        state = {}
-        pending = []
+        held = {}
+        banks_used = [0]
 
-        def small_step():
-            if pending:
-                pending.pop(0)()
-
-        bank_count = [0]
-
-        def next_bank():
-            tag = "bank%d" % (bank_count[0] % BANKS)
-            bank_count[0] += 1
-            return psum.tile([P, 512], F32, name=tag, tag=tag)
+        def next_bank(shape, dtype):
+            tag = "bank%d" % (banks_used[0] % BANKS)
+            banks_used[0] += 1
+            return psum.tile(shape, dtype, name=tag, tag=tag)
 
         def load(i):
             kind, u = units[i]
             if kind == "hidden":
-                for j in range(TILES):
-                    t = TILES * u + j
+                for t in range(TILES * u, TILES * (u + 1)):
                     nc.sync.dma_start(out=h_raw[:, t, :], in_=hidden_new[t * P : (t + 1) * P, :])
-                state[i, "raw"] = h_raw[:, TILES * u : TILES * (u + 1), :]
-                return
-            raw = rawp.tile([P, TILES, H], BF16, name="raw")
-            rows = weights[kind][u * UNIT : (u + 1) * UNIT, :]
-            nc.sync.dma_start(out=raw[:], in_=rows.rearrange("(j p) k -> p j k", j=TILES))
-            state[i, "raw"] = raw
-
-        def load_bias_lines():
-            for kind in ("addr", "forget", "write"):
-                first = FIRST_LINE[kind]
-                nc.scalar.dma_start(
-                    out=bias_lines[first : first + LINES, :], in_=biases[kind].rearrange("(c n) -> c n", n=LINE)
+                held[i, "raw"] = h_raw[:, TILES * u : TILES * (u + 1), :]
+            else:
+                raw = stream.tile([P, TILES, H], BF16, name="raw")
+                nc.sync.dma_start(out=raw[:], in_=weights[kind][slots(u), :].rearrange("(j p) k -> p j k", p=P))
+                held[i, "raw"] = raw
+            if i == 0:
+                for name, first in FIRST_LINE.items():
+                    nc.sync.dma_start(
+                        out=bias_lines[first : first + LINES, :],
+                        in_=biases[name].rearrange("(c n) -> c n", n=BANK),
+                    )
+            if kind == "forget" and u % (NUNIT // 2) == 0:
+                cols = slice(u * UNIT, u * UNIT + NSLOT // 2)
+                nc.sync.dma_start(
+                    out=memory[:, :, cols], in_=persistent_memory[:, cols].rearrange("(t p) c -> p t c", p=P)
                 )
 
-        def spread_bias(kind, unit_list, copy):
-            bank = next_bank()
-            for k, u in enumerate(unit_list):
-                line = FIRST_LINE[kind] + u // 2
+        def spread_bias(kind, pieces):
+            bank = next_bank([P, BANK], F32)
+            at = 0
+            for first, width in pieces:
+                line = FIRST_LINE[kind] + first // BANK
                 nc.tensor.matmul(
-                    bank[:, k * UNIT : (k + 1) * UNIT],
+                    bank[:, at : at + width],
                     lhsT=ident_bf[:, line : line + 1].to_broadcast([P, P]),
-                    rhs=bias_lines[:, (u % 2) * UNIT : (u % 2 + 1) * UNIT],
-                    start=True, stop=True,
+                    rhs=bias_lines[:, first % BANK : first % BANK + width],
+                    start=True,
+                    stop=True,
                 )
-            for k, u in enumerate(unit_list):
-                copy(out=bias_rows[kind][:, u * UNIT : (u + 1) * UNIT], in_=bank[:, k * UNIT : (k + 1) * UNIT])
+                at += width
+            at = 0
+            for first, width in pieces:
+                nc.scalar.copy(out=row_bias[kind][:, first : first + width], in_=bank[:, at : at + width])
+                at += width
 
-        def spread_line(kind, c, copy):
-            bank = next_bank()
-            line = FIRST_LINE[kind] + c
-            nc.tensor.matmul(
-                bank[:], lhsT=ident_bf[:, line : line + 1].to_broadcast([P, P]), rhs=bias_lines[:],
-                start=True, stop=True,
-            )
-            copy(out=bias_rows[kind][:, c * LINE : (c + 1) * LINE], in_=bank[:])
-
-        def turn_bias_lines():
-            tag = "bank%d" % (bank_count[0] % BANKS)
-            bank_count[0] += 1
-            turned = psum.tile([P, LINE // P, P], BF16, name=tag, tag=tag)
-            for j in range(LINE // P):
+        def turn_bias():
+            turned = next_bank([P, BANK // P, P], BF16)
+            for j in range(BANK // P):
                 nc.tensor.transpose(turned[:, j, :], bias_lines[:, j * P : (j + 1) * P], ident_bf[:])
-            views = {}
-            for kind in ("forget", "write"):
-                first = FIRST_LINE[kind]
-                views[kind] = turned[:, :, first : first + LINES].rearrange("p j c -> p c j")
-            cols = bias_cols[:].rearrange("p g (c j) -> p g c j", j=LINE // P)
-            halves = half_cols[:].rearrange("p (c j) -> p c j", j=LINE // P)
-            nc.vector.tensor_scalar(out=halves, in0=views["forget"], scalar1=0.5, scalar2=None, op0=ALU.mult)
-            if TANH_UNITS < NUNIT:
-                nc.vector.tensor_copy(out=cols[:, 0], in_=views["forget"])
-            nc.vector.tensor_copy(out=cols[:, 1], in_=views["write"])
-
-        def load_memory(lo, hi):
-            nc.sync.dma_start(
-                out=memory[:, :, lo:hi],
-                in_=persistent_memory[:, lo:hi].rearrange("(t p) c -> p t c", p=P),
+            gates = slice(FIRST_LINE["forget"], FIRST_LINE["write"] + LINES)
+            nc.vector.tensor_copy(out=col_bias[:, :, gates], in_=turned[:, :, gates])
+            forget = slice(FIRST_LINE["forget"], FIRST_LINE["forget"] + LINES)
+            nc.vector.tensor_scalar(
+                out=half_bias[:], in0=turned[:, :, forget], scalar1=0.5, scalar2=None, op0=ALU.mult
             )
 
-        def transpose_rows(i):
-            raw = state[i, "raw"]
-            banks = []
-            for j in range(TILES):
-                words = raw[:, j, :].bitcast(F32)
-                bank = next_bank()
-                view = bank[:].rearrange("p (g v r) -> p g v r", g=PASSES, v=2)
-                for g in range(PASSES):
-                    for v in range(2):
-                        nc.tensor.transpose(view[:, g, v, :], words[:, 256 * g + v : 256 * (g + 1) : 2], ident[:])
-                banks.append(bank)
-            state[i, "tbanks"] = banks
-
-        def copy_rows(i):
-            grouped = work.tile([P, PASSES * UNIT * 4], BF16, name="grouped", align_bytes=64)
-            words = grouped[:].bitcast(F32).rearrange("p (g r v) -> p g r v", g=PASSES, v=2)
-            for j in range(TILES):
-                src = state[i, "tbanks"][j][:].rearrange("p (g v r) -> p g r v", g=PASSES, v=2)
-                nc.scalar.copy(out=words[:, :, j * P : (j + 1) * P, :], in_=src)
-            state[i, "grouped"] = grouped
+        def transpose_tile(i, j):
+            words = held[i, "raw"][:, j, :].bitcast(F32)
+            bank = next_bank([P, PASSES, 2, P], F32)
+            for g in range(PASSES):
+                for v in range(2):
+                    nc.tensor.transpose(
+                        bank[:, g, v, :], words[:, PASS_WORDS * g + v : PASS_WORDS * (g + 1) : 2], ident[:]
+                    )
+            held[i, "turned", j] = bank
 
         def quantize(i):
             kind, u = units[i]
-            grouped = state[i, "grouped"]
+            grouped = work.tile([P, PASSES * UNIT * PACK], BF16, name="grouped", align_bytes=64)
+            words = grouped[:].bitcast(F32).rearrange("p (g r v) -> p g r v", g=PASSES, v=2)
+            for j in range(TILES):
+                nc.scalar.copy(
+                    out=words[:, :, j * P : (j + 1) * P, :],
+                    in_=held[i, "turned", j][:].rearrange("p g v r -> p g r v"),
+                )
             if kind == "hidden":
-                cols = slice(u * UNIT, (u + 1) * UNIT)
                 for g in range(PASSES):
                     nc.vector.quantize_mx(
-                        out=h_codes[:, g, cols].bitcast(E5M2),
-                        scales=h_scales[:, g, cols],
-                        in_=grouped[:, g * UNIT * 4 : (g + 1) * UNIT * 4],
+                        out=h_codes[:, g, slots(u)].bitcast(E5M2),
+                        scales=h_scales[:, g, slots(u)],
+                        in_=grouped[:, g * UNIT * PACK : (g + 1) * UNIT * PACK],
                     )
-                state["hq", u] = True
-                return
-            w_codes = work.tile([P, PASSES * UNIT], U32, name="w_codes", align_bytes=64)
-            w_scales = work.tile([P, PASSES * UNIT], U8, name="w_scales", align_bytes=64)
-            nc.vector.quantize_mx(out=w_codes[:].bitcast(E4M3), scales=w_scales[:], in_=grouped[:])
-            state[i, "codes"] = (w_codes, w_scales)
-            small_step()
+                rows = slice(TILES * u, TILES * (u + 1))
+                nc.vector.tensor_reduce(out=h_sum[:, rows], in_=h_raw[:, rows, :], axis=AXIS_X, op=ALU.add)
+            else:
+                w_codes = work.tile([P, PASSES * UNIT], U32, name="w_codes", align_bytes=64)
+                w_scales = work.tile([P, PASSES * UNIT], U8, name="w_scales", align_bytes=64)
+                nc.vector.quantize_mx(out=w_codes[:].bitcast(E4M3), scales=w_scales[:], in_=grouped[:])
+                held[i, "codes"] = (w_codes, w_scales)
 
-        def multiply(i, halves=(0, 1)):
-            kind, u = units[i]
-            w_codes, w_scales = state[i, "codes"]
-            banks = state.setdefault((i, "mbanks"), [])
-            for b in halves:
-                bank = next_bank()
-                if w_stationary(kind, u):
+        def multiply_token_form(i):
+            w_codes, w_scales = held[i, "codes"]
+            banks = []
+            for half in range(HALVES):
+                bank = next_bank([P, PAIR, UNIT], F32)
+                for tt in range(PAIR):
+                    tokens = slice((PAIR * half + tt) * P, (PAIR * half + tt + 1) * P)
                     for g in range(PASSES):
-                        cols = slice(g * UNIT + b * P, g * UNIT + (b + 1) * P)
                         nc.tensor.matmul_mx(
-                            out=bank[:],
-                            lhsT=w_codes[:, cols].bitcast(E4M3),
-                            lhsT_scale=w_scales[:, cols],
-                            rhs=h_codes[:, g, :].bitcast(E5M2),
-                            rhs_scale=h_scales[:, g, :],
+                            out=bank[:, tt, :],
+                            lhsT=h_codes[:, g, tokens].bitcast(E5M2),
+                            lhsT_scale=h_scales[:, g, tokens],
+                            rhs=w_codes[:, slots(g)].bitcast(E4M3),
+                            rhs_scale=w_scales[:, slots(g)],
                             start=(g == 0),
                             stop=(g == PASSES - 1),
                         )
-                else:
-                    for tt in range(2):
-                        t = 2 * b + tt
-                        for g in range(PASSES):
-                            cols = slice(g * UNIT, (g + 1) * UNIT)
-                            nc.tensor.matmul_mx(
-                                out=bank[:, tt * UNIT : (tt + 1) * UNIT],
-                                lhsT=h_codes[:, g, t * P : (t + 1) * P].bitcast(E5M2),
-                                lhsT_scale=h_scales[:, g, t * P : (t + 1) * P],
-                                rhs=w_codes[:, cols].bitcast(E4M3),
-                                rhs_scale=w_scales[:, cols],
-                                start=(g == 0),
-                                stop=(g == PASSES - 1),
-                            )
                 banks.append(bank)
+            return banks
 
-        def add_bias(i):
-            kind, u = units[i]
-            bias = bias_rows[kind][:, u * UNIT : (u + 1) * UNIT].unsqueeze(1).broadcast_to([P, 2, UNIT])
-            if kind != "addr":
-                gate = work.tile([P, NTOK, UNIT], F32, name="gate")
-                state[i, "gate"] = gate
-            for b in range(2):
-                sums = state[i, "mbanks"][b][:].rearrange("p (t c) -> p t c", t=2)
-                if kind == "addr":
-                    nc.vector.scalar_tensor_tensor(
-                        out=expo[:, u, 2 * b : 2 * b + 2, :], in0=sums, scalar=-1.0, in1=bias,
-                        op0=ALU.mult, op1=ALU.subtract,
+        def multiply_slot_form(i):
+            w_codes, w_scales = held[i, "codes"]
+            banks = []
+            for j in range(TILES):
+                bank = next_bank([P, B], F32)
+                for g in range(PASSES):
+                    cols = slice(g * UNIT + j * P, g * UNIT + (j + 1) * P)
+                    nc.tensor.matmul_mx(
+                        out=bank[:],
+                        lhsT=w_codes[:, cols].bitcast(E4M3),
+                        lhsT_scale=w_scales[:, cols],
+                        rhs=h_codes[:, g, :].bitcast(E5M2),
+                        rhs_scale=h_scales[:, g, :],
+                        start=(g == 0),
+                        stop=(g == PASSES - 1),
                     )
-                else:
-                    nc.vector.tensor_tensor(out=gate[:, 2 * b : 2 * b + 2, :], in0=sums, in1=bias, op=ALU.add)
-                small_step()
+                banks.append(bank)
+            return banks
 
-        def unit_max(i):
-            kind, u = units[i]
-            for b in range(2):
-                nc.vector.tensor_reduce(
-                    out=neg_max[:, 2 * b : 2 * b + 2, u], in_=expo[:, u, 2 * b : 2 * b + 2, :],
-                    axis=AXIS_X, op=ALU.min,
+        def bias_for_pair(kind, u):
+            return row_bias[kind][:, slots(u)].unsqueeze(1).broadcast_to([P, PAIR, UNIT])
+
+        def exponentials(u, banks):
+            for half in range(HALVES):
+                nc.vector.scalar_tensor_tensor(
+                    out=expo[:, u, pair(half), :], in0=banks[half][:], scalar=-1.0, in1=bias_for_pair("addr", u),
+                    op0=ALU.mult, op1=ALU.subtract,
                 )
-
-        def exponentials(i):
-            kind, u = units[i]
+            for half in range(HALVES):
+                nc.vector.tensor_reduce(
+                    out=neg_max[:, pair(half), u], in_=expo[:, u, pair(half), :], axis=AXIS_X, op=ALU.min
+                )
             for t in range(NTOK):
                 nc.scalar.activation(
                     out=expo[:, u, t, :], in_=expo[:, u, t, :], func=ACT.Exp, scale=-1.0,
                     bias=neg_max[:, t, u : u + 1], accum_out=exp_sum[:, t, u : u + 1],
                 )
 
-        def sigmoid_rows(i):
-            gate = state[i, "gate"]
-            for b in range(2):
-                rows = gate[:, 2 * b : 2 * b + 2, :]
-                if by_tanh(units[i][0], units[i][1]):
+        def softmax_coefficients():
+            def per_unit(column):
+                return column.unsqueeze(2).broadcast_to([P, NTOK, NUNIT])
+
+            row_neg_max = keep.tile([P, NTOK], F32)
+            nc.vector.tensor_reduce(out=row_neg_max[:], in_=neg_max[:], axis=AXIS_X, op=ALU.min)
+            gap = keep.tile([P, NTOK, NUNIT], F32)
+            nc.vector.tensor_tensor(out=gap[:], in0=per_unit(row_neg_max[:]), in1=neg_max[:], op=ALU.subtract)
+            rescale = keep.tile([P, NTOK, NUNIT], F32)
+            nc.scalar.activation(out=rescale[:], in_=gap[:], func=ACT.Exp)
+            unit_total = keep.tile([P, NTOK, NUNIT], F32)
+            nc.vector.tensor_tensor(out=unit_total[:], in0=exp_sum[:], in1=rescale[:], op=ALU.mult)
+            row_total = keep.tile([P, NTOK], F32)
+            nc.vector.tensor_reduce(out=row_total[:], in_=unit_total[:], axis=AXIS_X, op=ALU.add)
+            row_inverse = keep.tile([P, NTOK], F32)
+            nc.vector.reciprocal(out=row_inverse[:], in_=row_total[:])
+            row_factor = keep.tile([P, NTOK], F32)
+            nc.vector.scalar_tensor_tensor(
+                out=row_factor[:], in0=row_inverse[:], scalar=1.0 / H, in1=h_sum[:], op0=ALU.mult, op1=ALU.mult
+            )
+            nc.vector.tensor_tensor(out=coef[:], in0=rescale[:], in1=per_unit(row_factor[:]), op=ALU.mult)
+
+        def forget_times_memory(u, half, gate):
+            nc.vector.scalar_tensor_tensor(
+                out=result[:, u, pair(half), :], in0=gate, scalar=1.0 if by_tanh("forget", u) else 0.0,
+                in1=memory[:, pair(half), slots(u)], op0=ALU.add, op1=ALU.mult,
+            )
+
+        def forget_token_form(u, banks):
+            gate = work.tile([P, NTOK, UNIT], F32, name="gate")
+            for half in range(HALVES):
+                nc.vector.tensor_tensor(
+                    out=gate[:, pair(half), :], in0=banks[half][:], in1=bias_for_pair("forget", u), op=ALU.add
+                )
+            for half in range(HALVES):
+                rows = gate[:, pair(half), :]
+                if by_tanh("forget", u):
                     nc.scalar.activation(out=rows, in_=rows, func=ACT.Tanh, scale=0.5)
                 else:
                     nc.scalar.activation(out=rows, in_=rows, func=ACT.Sigmoid)
+            for half in range(HALVES):
+                forget_times_memory(u, half, gate[:, pair(half), :])
 
-        def sigmoid_cols(i):
+        def gate_slot_form(i, banks):
             kind, u = units[i]
             gate_t = work.tile([P, TILES, B], F32, name="gate_t")
             for j in range(TILES):
-                c = TILES * u + j
+                line, place = divmod(TILES * u + j, BANK // P)
                 if by_tanh(kind, u):
                     nc.scalar.activation(
-                        out=gate_t[:, j, :], in_=state[i, "mbanks"][j][:], func=ACT.Tanh, scale=0.5,
-                        bias=half_cols[:, c : c + 1],
+                        out=gate_t[:, j, :], in_=banks[j][:], func=ACT.Tanh, scale=0.5,
+                        bias=half_bias[:, place, line : line + 1],
                     )
                 else:
+                    line += FIRST_LINE[kind]
                     nc.scalar.activation(
-                        out=gate_t[:, j, :], in_=state[i, "mbanks"][j][:], func=ACT.Sigmoid,
-                        bias=bias_cols[:, 0 if kind == "forget" else 1, c : c + 1],
+                        out=gate_t[:, j, :], in_=banks[j][:], func=ACT.Sigmoid,
+                        bias=col_bias[:, place, line : line + 1],
                     )
-            state[i, "gate_t"] = gate_t
+            held[i, "gate_t"] = gate_t
 
-        def transpose_gate(i):
-            gate_t = state[i, "gate_t"]
-            banks = []
-            for b in range(2):
-                bank = next_bank()
-                view = bank[:].rearrange("p (t j m) -> p t j m", t=2, j=TILES)
-                for tt in range(2):
-                    t = 2 * b + tt
-                    for j in range(TILES):
-                        nc.tensor.transpose(view[:, tt, j, :], gate_t[:, j, t * P : (t + 1) * P], ident[:])
-                banks.append(bank)
-            state[i, "gbanks"] = banks
-
-        def gate_view(i, b):
+        def multiply(i):
             kind, u = units[i]
-            if w_stationary(kind, u):
-                return state[i, "gbanks"][b][:].rearrange("p (t c) -> p t c", t=2)
-            return state[i, "gate"][:, 2 * b : 2 * b + 2, :]
+            if slot_form(kind, u):
+                gate_slot_form(i, multiply_slot_form(i))
+            elif kind == "forget":
+                forget_token_form(u, multiply_token_form(i))
+            else:
+                exponentials(u, multiply_token_form(i))
+                if u == NUNIT - 1:
+                    softmax_coefficients()
 
-        def apply_gate(i):
-            kind, u = units[i]
-            if kind == "write":
-                while pending:
-                    small_step()
-                write_term = work.tile([P, NTOK, UNIT], F32, name="write_term", bufs=3)
-                state["write", u] = write_term
-            for b in range(2):
-                gate = gate_view(i, b)
-                if kind == "forget":
-                    nc.vector.scalar_tensor_tensor(
-                        out=forget_term[:, u, 2 * b : 2 * b + 2, :],
-                        in0=gate,
-                        scalar=1.0 if by_tanh(kind, u) else 0.0,
-                        in1=memory[:, 2 * b : 2 * b + 2, u * UNIT : (u + 1) * UNIT],
-                        op0=ALU.add, op1=ALU.mult,
-                    )
-                    small_step()
-                else:
-                    for tt in range(2):
-                        t = 2 * b + tt
-                        nc.vector.scalar_tensor_tensor(
-                            out=write_term[:, t, :], in0=gate[:, tt, :], scalar=coef[:, t, u : u + 1],
-                            in1=expo[:, u, t, :], op0=ALU.mult, op1=ALU.mult,
-                        )
-
-        def finish(u):
-            for b in range(2):
-                rows = slice(2 * b, 2 * b + 2)
+        def write_and_store(u, banks):
+            written = work.tile([P, NTOK, UNIT], F32, name="written")
+            for t in range(NTOK):
                 nc.vector.scalar_tensor_tensor(
-                    out=forget_term[:, u, rows, :], in0=forget_term[:, u, rows, :], scalar=0.5 if by_tanh("forget", u) else 1.0,
-                    in1=state["write", u][:, rows, :], op0=ALU.mult, op1=ALU.add,
+                    out=written[:, t, :], in0=banks[t // PAIR][:, t % PAIR, :], scalar=coef[:, t, u : u + 1],
+                    in1=expo[:, u, t, :], op0=ALU.mult, op1=ALU.mult,
                 )
+            for half in range(HALVES):
+                nc.vector.scalar_tensor_tensor(
+                    out=result[:, u, pair(half), :], in0=result[:, u, pair(half), :],
+                    scalar=0.5 if by_tanh("forget", u) else 1.0, in1=written[:, pair(half), :],
+                    op0=ALU.mult, op1=ALU.add,
+                )
+                tokens = slice(PAIR * half * P, PAIR * (half + 1) * P)
                 nc.sync.dma_start(
-                    out=out[2 * b * P : (2 * b + 2) * P, u * UNIT : (u + 1) * UNIT].rearrange("(t p) c -> p t c", p=P),
-                    in_=forget_term[:, u, rows, :],
+                    out=out[tokens, slots(u)].rearrange("(t p) c -> p t c", p=P), in_=result[:, u, pair(half), :]
                 )
 
-        def spread(col):
-            return col.unsqueeze(2).broadcast_to([P, NTOK, NUNIT])
+        def turn_gate(i):
+            kind, u = units[i]
+            gate_t = held[i, "gate_t"]
+            banks = []
+            for half in range(HALVES):
+                bank = next_bank([P, PAIR, UNIT], F32)
+                for tt in range(PAIR):
+                    t = PAIR * half + tt
+                    for j in range(TILES):
+                        nc.tensor.transpose(
+                            bank[:, tt, j * P : (j + 1) * P], gate_t[:, j, t * P : (t + 1) * P], ident[:]
+                        )
+                banks.append(bank)
+            if kind == "write":
+                write_and_store(u, banks)
+            else:
+                for half in range(HALVES):
+                    forget_times_memory(u, half, banks[half][:])
 
-        def softmax_gap():
-            pending.append(lambda: nc.vector.tensor_reduce(out=row_neg_max[:], in_=neg_max[:], axis=AXIS_X, op=ALU.min))
-            pending.append(lambda: nc.vector.tensor_tensor(
-                out=unit_gap[:], in0=spread(row_neg_max[:]), in1=neg_max[:], op=ALU.subtract))
+        count = len(units)
+        multiply_at = {}
+        turn_at = {}
+        for i, (kind, u) in enumerate(units):
+            shorter = 1 if i >= SHORT_FROM else 0
+            if kind != "hidden":
+                multiply_at.setdefault(i + MULTIPLY_LAG - shorter, []).append(i)
+            if slot_form(kind, u):
+                turn_at.setdefault(i + MULTIPLY_LAG + TURN_LAG - 2 * shorter, []).append(i)
+        token_forget = [(u * UNIT, UNIT) for u in range(NUNIT) if not slot_form("forget", u)]
+        first_multiply = min(multiply_at)
+        spread_at = {first_multiply + k // PAIR: token_forget[k : k + PAIR] for k in range(0, len(token_forget), PAIR)}
 
-        def softmax_factor():
-            while pending:
-                small_step()
-            nc.scalar.activation(out=unit_factor[:], in_=unit_gap[:], func=ACT.Exp)
-
-        def softmax_coef():
-            pending.append(lambda: nc.vector.tensor_tensor(
-                out=unit_weight[:], in0=exp_sum[:], in1=unit_factor[:], op=ALU.mult))
-            pending.append(lambda: nc.vector.tensor_reduce(
-                out=row_total[:], in_=unit_weight[:], axis=AXIS_X, op=ALU.add))
-            pending.append(lambda: nc.vector.reciprocal(out=row_inverse[:], in_=row_total[:]))
-            pending.append(lambda: nc.vector.scalar_tensor_tensor(
-                out=row_factor[:], in0=row_inverse[:], scalar=1.0 / H, in1=h_sum[:], op0=ALU.mult, op1=ALU.mult))
-            pending.append(lambda: nc.vector.tensor_tensor(
-                out=coef[:], in0=unit_factor[:], in1=spread(row_factor[:]), op=ALU.mult))
-
-        def row_sums(u):
-            rows = slice(TILES * u, TILES * (u + 1))
-            nc.vector.tensor_reduce(out=h_sum[:, rows], in_=h_raw[:, rows, :], axis=AXIS_X, op=ALU.add)
-
-        n = len(units)
-        first_forget = units.index(("forget", 0))
-        last_addr = units.index(("addr", NUNIT - 1))
-
-        def kind_of(i):
-            return units[i][0] if 0 <= i < n else "none"
-
-        def is_weight(i):
-            return kind_of(i) in weights
-
-        def is_cols(i):
-            return is_weight(i) and w_stationary(units[i][0], units[i][1])
-
-        def is_rows(i):
-            return is_weight(i) and not is_cols(i)
-
-        def is_gate_rows(i):
-            return is_rows(i) and kind_of(i) != "addr"
-
-        ahead = 10
-        loaded = [0]
-
-        def load_up_to(limit):
-            while loaded[0] < min(limit, n):
-                i = loaded[0]
-                load(i)
-                kind, u = units[i]
-                if kind == "forget" and u % 4 == 0:
-                    load_memory(u * UNIT, (u + 4) * UNIT)
-                loaded[0] += 1
-
-        def due(stage, s):
-            return [i for i in range(n) if i + (LAG2 if i >= SWITCH else LAG)[stage] == s]
-
-        load_bias_lines()
-        load_up_to(2 + ahead)
-        for c in range(LINES):
-            spread_line("addr", c, nc.scalar.copy if c % 2 == 0 else nc.vector.tensor_copy)
-        row_gates = [(kind, [u for u in range(NUNIT) if not w_stationary(kind, u)]) for kind in ("forget", "write")]
-        row_groups = [(kind, us[k : k + 2]) for kind, us in row_gates for k in range(0, len(us), 2)]
-        for s in range(n + max(LAG.values()) + 1):
-            if s % RUN == 0:
-                for r in range(RUN):
-                    if s + r < n:
-                        transpose_rows(s + r)
-                if s == 4:
-                    turn_bias_lines()
-                if 1 <= s <= len(row_groups):
-                    spread_bias(row_groups[s - 1][0], row_groups[s - 1][1], nc.scalar.copy)
-                if s >= n:
-                    for r in range(RUN):
-                        for i in due("mx", s + r):
-                            if is_weight(i):
-                                multiply(i)
-                for r in range(RUN):
-                    for i in due("rt", s + r):
-                        if is_cols(i):
-                            transpose_gate(i)
-                if s < n:
-                    if EARLY and s == 2:
-                        multiply(1, (0,))
-                    for r in range(RUN):
-                        for i in due("mx", s + r):
-                            if is_weight(i):
-                                multiply(i, (1,) if EARLY and i == 1 else (0, 1))
-            load_up_to(s + 1 + ahead)
-            if s == 0:
-                row_sums(0)
-            for i in due("bias", s):
-                if is_rows(i):
-                    add_bias(i)
-            for i in due("bias", s):
-                if kind_of(i) == "addr":
-                    unit_max(i)
-                if i == last_addr:
-                    softmax_gap()
-            if s < n:
-                copy_rows(s)
-            for i in due("act", s):
-                if kind_of(i) == "addr":
-                    exponentials(i)
-            if s - LAG["bias"] - 1 == last_addr:
-                softmax_factor()
-            for i in due("act", s):
-                if is_gate_rows(i):
-                    sigmoid_rows(i)
-            for i in due("sigc", s):
-                if is_cols(i):
-                    sigmoid_cols(i)
-            for i in due("appc", s):
-                if is_cols(i):
-                    apply_gate(i)
-            if s < n:
-                quantize(s)
-            if units[min(s, n - 1)] == ("hidden", 1):
-                row_sums(1)
-            if s - max(LAG["act"], LAG["bias"] + 1) == last_addr:
-                softmax_coef()
-            for i in due("appr", s):
-                if is_gate_rows(i):
-                    apply_gate(i)
-            for i in due("fin", s):
-                if kind_of(i) == "write":
-                    finish(units[i][1])
+        ahead = 2 + RAW_BUFS
+        for i in range(ahead):
+            load(i)
+        for step in range(max(turn_at) + 1):
+            if step < count:
+                for j in range(TILES):
+                    transpose_tile(step, j)
+                    if step == 0 and j == 0:
+                        for c in range(LINES):
+                            spread_bias("addr", [(c * BANK, BANK)])
+                quantize(step)
+            if step == first_multiply + 1:
+                turn_bias()
+            if step < count:
+                for i in turn_at.get(step, []):
+                    turn_gate(i)
+            for i in multiply_at.get(step, []):
+                multiply(i)
+            if step >= count:
+                for i in turn_at.get(step, []):
+                    turn_gate(i)
+            if step in spread_at:
+                spread_bias("forget", spread_at[step])
+            if step + ahead < count:
+                load(step + ahead)

@@ -29,14 +29,15 @@ NTOK = B // P
 PAIR = BANK // UNIT
 HALVES = NTOK // PAIR
 LINES = NSLOT // BANK
-FIRST_LINE = {"addr": 0, "forget": LINES, "write": 2 * LINES}
 
-ADDR_LEAD = 6
-FORGET_PERIOD = 4
-TANH_UNITS = 4
+ADDR_LEAD = 5
+SLOT_FORGET = 4
+FORGET_LINES = SLOT_FORGET * UNIT // BANK
+FIRST_LINE = {"addr": 0, "write": LINES, "forget": 2 * LINES}
+LINE_COUNT = {"addr": LINES, "write": LINES, "forget": FORGET_LINES}
+FORGET_BIAS_AFTER = 8
 MULTIPLY_LAG = 2
 TURN_LAG = 2
-SHORT_FROM = 18
 RAW_BUFS = 10
 WORK_BUFS = 4
 
@@ -57,10 +58,7 @@ def tile_persistentgrucell_pc_kernel(
     units += [("write", u) for u in range(NUNIT)]
 
     def slot_form(kind, u):
-        return kind == "write" or (kind == "forget" and u % FORGET_PERIOD == 1)
-
-    def by_tanh(kind, u):
-        return kind == "forget" and u < TANH_UNITS
+        return kind == "write" or (kind == "forget" and u < SLOT_FORGET)
 
     def slots(u):
         return slice(u * UNIT, (u + 1) * UNIT)
@@ -84,6 +82,7 @@ def tile_persistentgrucell_pc_kernel(
         h_codes = keep.tile([P, PASSES, B], U32, align_bytes=64)
         h_scales = keep.tile([P, PASSES, B], U8, align_bytes=64)
         h_sum = keep.tile([P, NTOK], F32)
+        h_unread = keep.tile([P, H], BF16)
         memory = keep.tile([P, NTOK, NSLOT], BF16)
         expo = keep.tile([P, NUNIT, NTOK, UNIT], F32)
         neg_max = keep.tile([P, NTOK, NUNIT], F32)
@@ -94,10 +93,9 @@ def tile_persistentgrucell_pc_kernel(
         bias_lines = keep.tile([P, BANK], BF16)
         nc.vector.memset(bias_lines[:], 0.0)
         addr_bias = keep.tile([P, NSLOT], BF16)
-        forget_bias = keep.tile([P, NSLOT], BF16)
-        row_bias = {"addr": addr_bias, "forget": forget_bias}
-        col_bias = keep.tile([P, BANK // P, 3 * LINES], F32)
-        half_bias = keep.tile([P, BANK // P, LINES], F32)
+        forget_bias = keep.tile([P, NSLOT - SLOT_FORGET * UNIT], BF16)
+        write_bias = keep.tile([P, BANK // P, LINES], F32)
+        half_forget_bias = keep.tile([P, BANK // P, FORGET_LINES], F32)
 
         held = {}
         banks_used = [0]
@@ -119,43 +117,39 @@ def tile_persistentgrucell_pc_kernel(
                 held[i, "raw"] = raw
             if i == 0:
                 for name, first in FIRST_LINE.items():
+                    lines = LINE_COUNT[name]
                     nc.sync.dma_start(
-                        out=bias_lines[first : first + LINES, :],
-                        in_=biases[name].rearrange("(c n) -> c n", n=BANK),
+                        out=bias_lines[first : first + lines, :],
+                        in_=biases[name][0 : lines * BANK].rearrange("(c n) -> c n", n=BANK),
                     )
+            if i == FORGET_BIAS_AFTER:
+                nc.sync.dma_start(out=forget_bias[:], in_=bforget[SLOT_FORGET * UNIT : NSLOT].partition_broadcast(P))
             if kind == "forget" and u % (NUNIT // 2) == 0:
                 cols = slice(u * UNIT, u * UNIT + NSLOT // 2)
                 nc.sync.dma_start(
                     out=memory[:, :, cols], in_=persistent_memory[:, cols].rearrange("(t p) c -> p t c", p=P)
                 )
 
-        def spread_bias(kind, pieces):
-            bank = next_bank([P, BANK], F32)
-            at = 0
-            for first, width in pieces:
-                line = FIRST_LINE[kind] + first // BANK
+        def spread_addr_bias():
+            for c in range(LINES):
+                bank = next_bank([P, BANK], F32)
+                line = FIRST_LINE["addr"] + c
                 nc.tensor.matmul(
-                    bank[:, at : at + width],
-                    lhsT=ident_bf[:, line : line + 1].to_broadcast([P, P]),
-                    rhs=bias_lines[:, first % BANK : first % BANK + width],
-                    start=True,
-                    stop=True,
+                    bank[:], lhsT=ident_bf[:, line : line + 1].to_broadcast([P, P]), rhs=bias_lines[:],
+                    start=True, stop=True,
                 )
-                at += width
-            at = 0
-            for first, width in pieces:
-                nc.scalar.copy(out=row_bias[kind][:, first : first + width], in_=bank[:, at : at + width])
-                at += width
+                nc.vector.tensor_copy(out=addr_bias[:, c * BANK : (c + 1) * BANK], in_=bank[:])
 
         def turn_bias():
             turned = next_bank([P, BANK // P, P], BF16)
             for j in range(BANK // P):
                 nc.tensor.transpose(turned[:, j, :], bias_lines[:, j * P : (j + 1) * P], ident_bf[:])
-            gates = slice(FIRST_LINE["forget"], FIRST_LINE["write"] + LINES)
-            nc.vector.tensor_copy(out=col_bias[:, :, gates], in_=turned[:, :, gates])
-            forget = slice(FIRST_LINE["forget"], FIRST_LINE["forget"] + LINES)
+            first = FIRST_LINE["write"]
+            nc.vector.tensor_copy(out=write_bias[:], in_=turned[:, :, first : first + LINES])
+            first = FIRST_LINE["forget"]
             nc.vector.tensor_scalar(
-                out=half_bias[:], in0=turned[:, :, forget], scalar1=0.5, scalar2=None, op0=ALU.mult
+                out=half_forget_bias[:], in0=turned[:, :, first : first + FORGET_LINES],
+                scalar1=0.5, scalar2=None, op0=ALU.mult,
             )
 
         def transpose_tile(i, j):
@@ -184,8 +178,11 @@ def tile_persistentgrucell_pc_kernel(
                         scales=h_scales[:, g, slots(u)],
                         in_=grouped[:, g * UNIT * PACK : (g + 1) * UNIT * PACK],
                     )
-                rows = slice(TILES * u, TILES * (u + 1))
-                nc.vector.tensor_reduce(out=h_sum[:, rows], in_=h_raw[:, rows, :], axis=AXIS_X, op=ALU.add)
+                for t in range(TILES * u, TILES * (u + 1)):
+                    nc.vector.tensor_scalar(
+                        out=h_unread[:], in0=h_raw[:, t, :], scalar1=1.0, scalar2=None,
+                        op0=ALU.mult, op1=ALU.add, accum_out=h_sum[:, t : t + 1],
+                    )
             else:
                 w_codes = work.tile([P, PASSES * UNIT], U32, name="w_codes", align_bytes=64)
                 w_scales = work.tile([P, PASSES * UNIT], U8, name="w_scales", align_bytes=64)
@@ -231,14 +228,14 @@ def tile_persistentgrucell_pc_kernel(
                 banks.append(bank)
             return banks
 
-        def bias_for_pair(kind, u):
-            return row_bias[kind][:, slots(u)].unsqueeze(1).broadcast_to([P, PAIR, UNIT])
+        def for_pair(bias):
+            return bias.unsqueeze(1).broadcast_to([P, PAIR, UNIT])
 
         def exponentials(u, banks):
             for half in range(HALVES):
                 nc.vector.scalar_tensor_tensor(
-                    out=expo[:, u, pair(half), :], in0=banks[half][:], scalar=-1.0, in1=bias_for_pair("addr", u),
-                    op0=ALU.mult, op1=ALU.subtract,
+                    out=expo[:, u, pair(half), :], in0=banks[half][:], scalar=-1.0,
+                    in1=for_pair(addr_bias[:, slots(u)]), op0=ALU.mult, op1=ALU.subtract,
                 )
             for half in range(HALVES):
                 nc.vector.tensor_reduce(
@@ -272,42 +269,33 @@ def tile_persistentgrucell_pc_kernel(
             )
             nc.vector.tensor_tensor(out=coef[:], in0=rescale[:], in1=per_unit(row_factor[:]), op=ALU.mult)
 
-        def forget_times_memory(u, half, gate):
-            nc.vector.scalar_tensor_tensor(
-                out=result[:, u, pair(half), :], in0=gate, scalar=1.0 if by_tanh("forget", u) else 0.0,
-                in1=memory[:, pair(half), slots(u)], op0=ALU.add, op1=ALU.mult,
-            )
-
         def forget_token_form(u, banks):
             gate = work.tile([P, NTOK, UNIT], F32, name="gate")
+            bias = for_pair(forget_bias[:, slots(u - SLOT_FORGET)])
+            for half in range(HALVES):
+                nc.vector.tensor_tensor(out=gate[:, pair(half), :], in0=banks[half][:], in1=bias, op=ALU.add)
+            for half in range(HALVES):
+                nc.scalar.activation(out=gate[:, pair(half), :], in_=gate[:, pair(half), :], func=ACT.Sigmoid)
             for half in range(HALVES):
                 nc.vector.tensor_tensor(
-                    out=gate[:, pair(half), :], in0=banks[half][:], in1=bias_for_pair("forget", u), op=ALU.add
+                    out=result[:, u, pair(half), :], in0=gate[:, pair(half), :],
+                    in1=memory[:, pair(half), slots(u)], op=ALU.mult,
                 )
-            for half in range(HALVES):
-                rows = gate[:, pair(half), :]
-                if by_tanh("forget", u):
-                    nc.scalar.activation(out=rows, in_=rows, func=ACT.Tanh, scale=0.5)
-                else:
-                    nc.scalar.activation(out=rows, in_=rows, func=ACT.Sigmoid)
-            for half in range(HALVES):
-                forget_times_memory(u, half, gate[:, pair(half), :])
 
         def gate_slot_form(i, banks):
             kind, u = units[i]
             gate_t = work.tile([P, TILES, B], F32, name="gate_t")
             for j in range(TILES):
                 line, place = divmod(TILES * u + j, BANK // P)
-                if by_tanh(kind, u):
+                if kind == "forget":
                     nc.scalar.activation(
                         out=gate_t[:, j, :], in_=banks[j][:], func=ACT.Tanh, scale=0.5,
-                        bias=half_bias[:, place, line : line + 1],
+                        bias=half_forget_bias[:, place, line : line + 1],
                     )
                 else:
-                    line += FIRST_LINE[kind]
                     nc.scalar.activation(
                         out=gate_t[:, j, :], in_=banks[j][:], func=ACT.Sigmoid,
-                        bias=col_bias[:, place, line : line + 1],
+                        bias=write_bias[:, place, line : line + 1],
                     )
             held[i, "gate_t"] = gate_t
 
@@ -332,7 +320,7 @@ def tile_persistentgrucell_pc_kernel(
             for half in range(HALVES):
                 nc.vector.scalar_tensor_tensor(
                     out=result[:, u, pair(half), :], in0=result[:, u, pair(half), :],
-                    scalar=0.5 if by_tanh("forget", u) else 1.0, in1=written[:, pair(half), :],
+                    scalar=0.5 if slot_form("forget", u) else 1.0, in1=written[:, pair(half), :],
                     op0=ALU.mult, op1=ALU.add,
                 )
                 tokens = slice(PAIR * half * P, PAIR * (half + 1) * P)
@@ -357,43 +345,48 @@ def tile_persistentgrucell_pc_kernel(
                 write_and_store(u, banks)
             else:
                 for half in range(HALVES):
-                    forget_times_memory(u, half, banks[half][:])
+                    nc.vector.scalar_tensor_tensor(
+                        out=result[:, u, pair(half), :], in0=banks[half][:], scalar=1.0,
+                        in1=memory[:, pair(half), slots(u)], op0=ALU.add, op1=ALU.mult,
+                    )
 
         count = len(units)
         multiply_at = {}
         turn_at = {}
         for i, (kind, u) in enumerate(units):
-            shorter = 1 if i >= SHORT_FROM else 0
+            shorter = 1 if kind == "write" else 0
             if kind != "hidden":
                 multiply_at.setdefault(i + MULTIPLY_LAG - shorter, []).append(i)
             if slot_form(kind, u):
                 turn_at.setdefault(i + MULTIPLY_LAG + TURN_LAG - 2 * shorter, []).append(i)
-        token_forget = [(u * UNIT, UNIT) for u in range(NUNIT) if not slot_form("forget", u)]
         first_multiply = min(multiply_at)
-        spread_at = {first_multiply + k // PAIR: token_forget[k : k + PAIR] for k in range(0, len(token_forget), PAIR)}
 
         ahead = 2 + RAW_BUFS
         for i in range(ahead):
             load(i)
-        for step in range(max(turn_at) + 1):
-            if step < count:
-                for j in range(TILES):
-                    transpose_tile(step, j)
-                    if step == 0 and j == 0:
-                        for c in range(LINES):
-                            spread_bias("addr", [(c * BANK, BANK)])
-                quantize(step)
-            if step == first_multiply + 1:
-                turn_bias()
-            if step < count:
-                for i in turn_at.get(step, []):
-                    turn_gate(i)
-            for i in multiply_at.get(step, []):
-                multiply(i)
-            if step >= count:
-                for i in turn_at.get(step, []):
-                    turn_gate(i)
-            if step in spread_at:
-                spread_bias("forget", spread_at[step])
-            if step + ahead < count:
-                load(step + ahead)
+        paired = range(units.index(("forget", 0)), units.index(("forget", NUNIT - 1)))
+        step = 0
+        while step <= max(turn_at):
+            run = [step, step + 1] if step in paired else [step]
+            for s in run:
+                if s < count:
+                    for j in range(TILES):
+                        transpose_tile(s, j)
+                        if s == 0 and j == 0:
+                            spread_addr_bias()
+                    quantize(s)
+                if s == first_multiply + 1:
+                    turn_bias()
+            for s in run:
+                if s < count:
+                    for i in turn_at.get(s, []):
+                        turn_gate(i)
+            for s in run:
+                for i in multiply_at.get(s, []):
+                    multiply(i)
+                if s >= count:
+                    for i in turn_at.get(s, []):
+                        turn_gate(i)
+                if s + ahead < count:
+                    load(s + ahead)
+            step += len(run)

from contextlib import ExitStack

import concourse.mybir as mybir
from concourse.masks import make_identity

B, H, NSLOT = 512, 1024, 2048
FLOPS = 3 * 2 * B * H * NSLOT

F32 = mybir.dt.float32
BF16 = mybir.dt.bfloat16
U32 = mybir.dt.uint32
U8 = mybir.dt.uint8
E4M3 = mybir.dt.float8_e4m3fn_x4
E5M2 = mybir.dt.float8_e5m2_x4
ALU = mybir.AluOpType
ACT = mybir.ActivationFunctionType
AXIS_X = mybir.AxisListType.X

P = 128
PACK = 4
PASSES = H // (P * PACK)
PASS_WORDS = P * PACK // 2
BANK = 512
BANKS = 8
UNIT = 256
TILES = UNIT // P
NUNIT = NSLOT // UNIT
NTOK = B // P
PAIR = BANK // UNIT
HALVES = NTOK // PAIR
LINES = NSLOT // BANK

ADDR_LEAD = 5
SLOT_FORGET = 4
FORGET_LINES = SLOT_FORGET * UNIT // BANK
FIRST_LINE = {"addr": 0, "write": LINES, "forget": 2 * LINES}
LINE_COUNT = {"addr": LINES, "write": LINES, "forget": FORGET_LINES}
FORGET_BIAS_AFTER = 8
MULTIPLY_LAG = 2
TURN_LAG = 2
RAW_BUFS = 10
WORK_BUFS = 4


def tile_persistentgrucell_pc_kernel(
    tc, hidden_new, persistent_memory, Waddr, baddr, Wwrite, bwrite, Wforget, bforget, out
):
    nc = tc.nc
    weights = {"addr": Waddr, "write": Wwrite, "forget": Wforget}
    biases = {"addr": baddr, "write": bwrite, "forget": bforget}

    units = [("hidden", 0), ("addr", 0), ("hidden", 1)]
    units += [("addr", u) for u in range(1, ADDR_LEAD)]
    for u in range(NUNIT):
        units.append(("forget", u))
        if ADDR_LEAD + u < NUNIT:
            units.append(("addr", ADDR_LEAD + u))
    units += [("write", u) for u in range(NUNIT)]

    def slot_form(kind, u):
        return kind == "write" or (kind == "forget" and u < SLOT_FORGET)

    def slots(u):
        return slice(u * UNIT, (u + 1) * UNIT)

    def pair(half):
        return slice(PAIR * half, PAIR * (half + 1))

    with ExitStack() as ctx:
        keep = ctx.enter_context(tc.tile_pool(name="keep", bufs=1))
        stream = ctx.enter_context(tc.tile_pool(name="stream", bufs=RAW_BUFS))
        work = ctx.enter_context(tc.tile_pool(name="work", bufs=WORK_BUFS))
        psum = ctx.enter_context(tc.psum_pool(name="psum", bufs=1))
        ctx.enter_context(tc.manual_schedule(engines={mybir.EngineType.PE, mybir.EngineType.SP}))

        ident = keep.tile([P, P], F32)
        make_identity(nc, ident[:])
        ident_bf = keep.tile([P, P], BF16)
        make_identity(nc, ident_bf[:])

        h_raw = keep.tile([P, NTOK, H], BF16)
        h_codes = keep.tile([P, PASSES, B], U32, align_bytes=64)
        h_scales = keep.tile([P, PASSES, B], U8, align_bytes=64)
        h_sum = keep.tile([P, NTOK], F32)
        h_unread = keep.tile([P, H], BF16)
        memory = keep.tile([P, NTOK, NSLOT], BF16)
        expo = keep.tile([P, NUNIT, NTOK, UNIT], F32)
        neg_max = keep.tile([P, NTOK, NUNIT], F32)
        exp_sum = keep.tile([P, NTOK, NUNIT], F32)
        coef = keep.tile([P, NTOK, NUNIT], F32)
        result = keep.tile([P, NUNIT, NTOK, UNIT], F32)

        bias_lines = keep.tile([P, BANK], BF16)
        nc.vector.memset(bias_lines[:], 0.0)
        addr_bias = keep.tile([P, NSLOT], BF16)
        forget_bias = keep.tile([P, NSLOT - SLOT_FORGET * UNIT], BF16)
        write_bias = keep.tile([P, BANK // P, LINES], F32)
        half_forget_bias = keep.tile([P, BANK // P, FORGET_LINES], F32)

        held = {}
        banks_used = [0]

        def next_bank(shape, dtype):
            tag = "bank%d" % (banks_used[0] % BANKS)
            banks_used[0] += 1
            return psum.tile(shape, dtype, name=tag, tag=tag)

        def load(i):
            kind, u = units[i]
            if kind == "hidden":
                for t in range(TILES * u, TILES * (u + 1)):
                    nc.sync.dma_start(out=h_raw[:, t, :], in_=hidden_new[t * P : (t + 1) * P, :])
                held[i, "raw"] = h_raw[:, TILES * u : TILES * (u + 1), :]
            else:
                raw = stream.tile([P, TILES, H], BF16, name="raw")
                nc.sync.dma_start(out=raw[:], in_=weights[kind][slots(u), :].rearrange("(j p) k -> p j k", p=P))
                held[i, "raw"] = raw
            if i == 0:
                for name, first in FIRST_LINE.items():
                    lines = LINE_COUNT[name]
                    nc.sync.dma_start(
                        out=bias_lines[first : first + lines, :],
                        in_=biases[name][0 : lines * BANK].rearrange("(c n) -> c n", n=BANK),
                    )
            if i == FORGET_BIAS_AFTER:
                nc.sync.dma_start(out=forget_bias[:], in_=bforget[SLOT_FORGET * UNIT : NSLOT].partition_broadcast(P))
            if kind == "forget" and u % (NUNIT // 2) == 0:
                cols = slice(u * UNIT, u * UNIT + NSLOT // 2)
                nc.sync.dma_start(
                    out=memory[:, :, cols], in_=persistent_memory[:, cols].rearrange("(t p) c -> p t c", p=P)
                )

        def spread_addr_bias():
            for c in range(LINES):
                bank = next_bank([P, BANK], F32)
                line = FIRST_LINE["addr"] + c
                nc.tensor.matmul(
                    bank[:], lhsT=ident_bf[:, line : line + 1].to_broadcast([P, P]), rhs=bias_lines[:],
                    start=True, stop=True,
                )
                nc.vector.tensor_copy(out=addr_bias[:, c * BANK : (c + 1) * BANK], in_=bank[:])

        def turn_bias():
            turned = next_bank([P, BANK // P, P], BF16)
            for j in range(BANK // P):
                nc.tensor.transpose(turned[:, j, :], bias_lines[:, j * P : (j + 1) * P], ident_bf[:])
            first = FIRST_LINE["write"]
            nc.vector.tensor_copy(out=write_bias[:], in_=turned[:, :, first : first + LINES])
            first = FIRST_LINE["forget"]
            nc.vector.tensor_scalar(
                out=half_forget_bias[:], in0=turned[:, :, first : first + FORGET_LINES],
                scalar1=0.5, scalar2=None, op0=ALU.mult,
            )

        def transpose_tile(i, j):
            words = held[i, "raw"][:, j, :].bitcast(F32)
            bank = next_bank([P, PASSES, 2, P], F32)
            for g in range(PASSES):
                for v in range(2):
                    nc.tensor.transpose(
                        bank[:, g, v, :], words[:, PASS_WORDS * g + v : PASS_WORDS * (g + 1) : 2], ident[:]
                    )
            held[i, "turned", j] = bank

        def quantize(i):
            kind, u = units[i]
            grouped = work.tile([P, PASSES * UNIT * PACK], BF16, name="grouped", align_bytes=64)
            words = grouped[:].bitcast(F32).rearrange("p (g r v) -> p g r v", g=PASSES, v=2)
            for j in range(TILES):
                nc.scalar.copy(
                    out=words[:, :, j * P : (j + 1) * P, :],
                    in_=held[i, "turned", j][:].rearrange("p g v r -> p g r v"),
                )
            if kind == "hidden":
                for g in range(PASSES):
                    nc.vector.quantize_mx(
                        out=h_codes[:, g, slots(u)].bitcast(E5M2),
                        scales=h_scales[:, g, slots(u)],
                        in_=grouped[:, g * UNIT * PACK : (g + 1) * UNIT * PACK],
                    )
                for t in range(TILES * u, TILES * (u + 1)):
                    nc.vector.tensor_scalar(
                        out=h_unread[:], in0=h_raw[:, t, :], scalar1=1.0, scalar2=None,
                        op0=ALU.mult, op1=ALU.add, accum_out=h_sum[:, t : t + 1],
                    )
            else:
                w_codes = work.tile([P, PASSES * UNIT], U32, name="w_codes", align_bytes=64)
                w_scales = work.tile([P, PASSES * UNIT], U8, name="w_scales", align_bytes=64)
                nc.vector.quantize_mx(out=w_codes[:].bitcast(E4M3), scales=w_scales[:], in_=grouped[:])
                held[i, "codes"] = (w_codes, w_scales)

        def multiply_token_form(i):
            w_codes, w_scales = held[i, "codes"]
            banks = []
            for half in range(HALVES):
                bank = next_bank([P, PAIR, UNIT], F32)
                for tt in range(PAIR):
                    tokens = slice((PAIR * half + tt) * P, (PAIR * half + tt + 1) * P)
                    for g in range(PASSES):
                        nc.tensor.matmul_mx(
                            out=bank[:, tt, :],
                            lhsT=h_codes[:, g, tokens].bitcast(E5M2),
                            lhsT_scale=h_scales[:, g, tokens],
                            rhs=w_codes[:, slots(g)].bitcast(E4M3),
                            rhs_scale=w_scales[:, slots(g)],
                            start=(g == 0),
                            stop=(g == PASSES - 1),
                        )
                banks.append(bank)
            return banks

        def multiply_slot_form(i):
            w_codes, w_scales = held[i, "codes"]
            banks = []
            for j in range(TILES):
                bank = next_bank([P, B], F32)
                for g in range(PASSES):
                    cols = slice(g * UNIT + j * P, g * UNIT + (j + 1) * P)
                    nc.tensor.matmul_mx(
                        out=bank[:],
                        lhsT=w_codes[:, cols].bitcast(E4M3),
                        lhsT_scale=w_scales[:, cols],
                        rhs=h_codes[:, g, :].bitcast(E5M2),
                        rhs_scale=h_scales[:, g, :],
                        start=(g == 0),
                        stop=(g == PASSES - 1),
                    )
                banks.append(bank)
            return banks

        def for_pair(bias):
            return bias.unsqueeze(1).broadcast_to([P, PAIR, UNIT])

        def exponentials(u, banks):
            for half in range(HALVES):
                nc.vector.scalar_tensor_tensor(
                    out=expo[:, u, pair(half), :], in0=banks[half][:], scalar=-1.0,
                    in1=for_pair(addr_bias[:, slots(u)]), op0=ALU.mult, op1=ALU.subtract,
                )
            for half in range(HALVES):
                nc.vector.tensor_reduce(
                    out=neg_max[:, pair(half), u], in_=expo[:, u, pair(half), :], axis=AXIS_X, op=ALU.min
                )
            for t in range(NTOK):
                nc.scalar.activation(
                    out=expo[:, u, t, :], in_=expo[:, u, t, :], func=ACT.Exp, scale=-1.0,
                    bias=neg_max[:, t, u : u + 1], accum_out=exp_sum[:, t, u : u + 1],
                )

        def softmax_coefficients():
            def per_unit(column):
                return column.unsqueeze(2).broadcast_to([P, NTOK, NUNIT])

            row_neg_max = keep.tile([P, NTOK], F32)
            nc.vector.tensor_reduce(out=row_neg_max[:], in_=neg_max[:], axis=AXIS_X, op=ALU.min)
            gap = keep.tile([P, NTOK, NUNIT], F32)
            nc.vector.tensor_tensor(out=gap[:], in0=per_unit(row_neg_max[:]), in1=neg_max[:], op=ALU.subtract)
            rescale = keep.tile([P, NTOK, NUNIT], F32)
            nc.scalar.activation(out=rescale[:], in_=gap[:], func=ACT.Exp)
            unit_total = keep.tile([P, NTOK, NUNIT], F32)
            nc.vector.tensor_tensor(out=unit_total[:], in0=exp_sum[:], in1=rescale[:], op=ALU.mult)
            row_total = keep.tile([P, NTOK], F32)
            nc.vector.tensor_reduce(out=row_total[:], in_=unit_total[:], axis=AXIS_X, op=ALU.add)
            row_inverse = keep.tile([P, NTOK], F32)
            nc.vector.reciprocal(out=row_inverse[:], in_=row_total[:])
            row_factor = keep.tile([P, NTOK], F32)
            nc.vector.scalar_tensor_tensor(
                out=row_factor[:], in0=row_inverse[:], scalar=1.0 / H, in1=h_sum[:], op0=ALU.mult, op1=ALU.mult
            )
            nc.vector.tensor_tensor(out=coef[:], in0=rescale[:], in1=per_unit(row_factor[:]), op=ALU.mult)

        def forget_token_form(u, banks):
            gate = work.tile([P, NTOK, UNIT], F32, name="gate")
            bias = for_pair(forget_bias[:, slots(u - SLOT_FORGET)])
            for half in range(HALVES):
                nc.vector.tensor_tensor(out=gate[:, pair(half), :], in0=banks[half][:], in1=bias, op=ALU.add)
            for half in range(HALVES):
                nc.scalar.activation(out=gate[:, pair(half), :], in_=gate[:, pair(half), :], func=ACT.Sigmoid)
            for half in range(HALVES):
                nc.vector.tensor_tensor(
                    out=result[:, u, pair(half), :], in0=gate[:, pair(half), :],
                    in1=memory[:, pair(half), slots(u)], op=ALU.mult,
                )

        def gate_slot_form(i, banks):
            kind, u = units[i]
            gate_t = work.tile([P, TILES, B], F32, name="gate_t")
            for j in range(TILES):
                line, place = divmod(TILES * u + j, BANK // P)
                if kind == "forget":
                    nc.scalar.activation(
                        out=gate_t[:, j, :], in_=banks[j][:], func=ACT.Tanh, scale=0.5,
                        bias=half_forget_bias[:, place, line : line + 1],
                    )
                else:
                    nc.scalar.activation(
                        out=gate_t[:, j, :], in_=banks[j][:], func=ACT.Sigmoid,
                        bias=write_bias[:, place, line : line + 1],
                    )
            held[i, "gate_t"] = gate_t

        def multiply(i):
            kind, u = units[i]
            if slot_form(kind, u):
                gate_slot_form(i, multiply_slot_form(i))
            elif kind == "forget":
                forget_token_form(u, multiply_token_form(i))
            else:
                exponentials(u, multiply_token_form(i))
                if u == NUNIT - 1:
                    softmax_coefficients()

        def write_and_store(u, banks):
            written = work.tile([P, NTOK, UNIT], F32, name="written")
            for t in range(NTOK):
                nc.vector.scalar_tensor_tensor(
                    out=written[:, t, :], in0=banks[t // PAIR][:, t % PAIR, :], scalar=coef[:, t, u : u + 1],
                    in1=expo[:, u, t, :], op0=ALU.mult, op1=ALU.mult,
                )
            for half in range(HALVES):
                nc.vector.scalar_tensor_tensor(
                    out=result[:, u, pair(half), :], in0=result[:, u, pair(half), :],
                    scalar=0.5 if slot_form("forget", u) else 1.0, in1=written[:, pair(half), :],
                    op0=ALU.mult, op1=ALU.add,
                )
                tokens = slice(PAIR * half * P, PAIR * (half + 1) * P)
                nc.sync.dma_start(
                    out=out[tokens, slots(u)].rearrange("(t p) c -> p t c", p=P), in_=result[:, u, pair(half), :]
                )

        def turn_gate(i):
            kind, u = units[i]
            gate_t = held[i, "gate_t"]
            banks = []
            for half in range(HALVES):
                bank = next_bank([P, PAIR, UNIT], F32)
                for tt in range(PAIR):
                    t = PAIR * half + tt
                    for j in range(TILES):
                        nc.tensor.transpose(
                            bank[:, tt, j * P : (j + 1) * P], gate_t[:, j, t * P : (t + 1) * P], ident[:]
                        )
                banks.append(bank)
            if kind == "write":
                write_and_store(u, banks)
            else:
                for half in range(HALVES):
                    nc.vector.scalar_tensor_tensor(
                        out=result[:, u, pair(half), :], in0=banks[half][:], scalar=1.0,
                        in1=memory[:, pair(half), slots(u)], op0=ALU.add, op1=ALU.mult,
                    )

        count = len(units)
        multiply_at = {}
        turn_at = {}
        for i, (kind, u) in enumerate(units):
            shorter = 1 if kind == "write" else 0
            if kind != "hidden":
                multiply_at.setdefault(i + MULTIPLY_LAG - shorter, []).append(i)
            if slot_form(kind, u):
                turn_at.setdefault(i + MULTIPLY_LAG + TURN_LAG - 2 * shorter, []).append(i)
        first_multiply = min(multiply_at)

        ahead = 2 + RAW_BUFS
        for i in range(ahead):
            load(i)
        paired = range(units.index(("forget", 0)), units.index(("forget", NUNIT - 1)))
        step = 0
        while step <= max(turn_at):
            run = [step, step + 1] if step in paired else [step]
            for s in run:
                if s < count:
                    for j in range(TILES):
                        transpose_tile(s, j)
                        if s == 0 and j == 0:
                            spread_addr_bias()
                    quantize(s)
                if s == first_multiply + 1:
                    turn_bias()
            for s in run:
                if s < count:
                    for i in turn_at.get(s, []):
                        turn_gate(i)
            for s in run:
                for i in multiply_at.get(s, []):
                    multiply(i)
                if s >= count:
                    for i in turn_at.get(s, []):
                        turn_gate(i)
                if s + ahead < count:
                    load(s + ahead)
            step += len(run)
